import numpy as np
import ml_dtypes


def mxq(x, axis, fmt="e4m3"):
    dtype, down = {"e4m3": (ml_dtypes.float8_e4m3fn, 7), "e5m2": (ml_dtypes.float8_e5m2, 14)}[fmt]
    v = np.moveaxis(np.asarray(x, np.float32).astype(ml_dtypes.bfloat16).astype(np.float64), axis, -1)
    blocks = v.reshape(v.shape[:-1] + (-1, 32))
    amax = np.abs(blocks).max(-1, keepdims=True)
    byte = np.maximum(np.where(amax > 0, np.frexp(amax)[1] - 1 + 127, 0) - down, 1)
    scale = np.exp2(byte - 127.0)
    codes = (blocks / scale).astype(np.float32).astype(dtype).astype(np.float64)
    return np.moveaxis((codes * scale).reshape(v.shape), -1, axis)


WIDE = False


def mx_kscale(k):
    if not WIDE:
        return np.ones(k)
    levels = np.array([10, -10, 5, -5, 0])
    a = np.random.permutation(np.resize(levels, k // 512 * 4)).reshape(k // 512, 4)
    idx = np.arange(k)
    return np.exp2(a[idx // 512, idx % 128 // 32])


BF16 = ml_dtypes.bfloat16


def bf(x):
    return np.asarray(x, np.float32).astype(BF16)


def f64(x):
    return np.asarray(x).astype(np.float64)


B, CIN, H, W, CR, COUT, SP, K = 4, 512, 32, 32, 512, 1024, 32, 7
PAD = K // 2
KK = K * K
HN = COUT // SP
HW = H * W
OFFS = [(dy, dx) for dy in range(K) for dx in range(K)]


def setup_inputs():
    s = mx_kscale(CIN)
    return {
        "logits": bf(np.random.standard_normal((B, HN, KK, HW)) * 1.5),
        "x": bf(np.random.standard_normal((B, CIN, H, W)) * s[None, :, None, None]),
        "w3c": bf(np.random.standard_normal((COUT, CIN)) * 2.0 / np.sqrt(CIN) / s[None, :]),
        "b3c": bf(np.random.standard_normal(COUT) * 0.5),
    }


def reference(logits, x, w3c, b3c):
    x3 = (mxq(f64(w3c), 1, "e4m3") @ mxq(f64(x).reshape(B, CIN, HW), 1, "e4m3")) + f64(b3c)[None, :, None]
    x3 = x3.reshape(B, COUT, H, W)
    lg = f64(logits)
    e = np.exp(lg - lg.max(axis=2, keepdims=True))
    wgt = (e / e.sum(axis=2, keepdims=True)).reshape(B, HN, KK, H, W)
    x3p = np.pad(x3, ((0, 0), (0, 0), (PAD, PAD), (PAD, PAD)), mode="reflect")
    acc = np.zeros((B, HN, SP, H, W))
    for k, (dy, dx) in enumerate(OFFS):
        patch = x3p[:, :, dy:dy + H, dx:dx + W].reshape(B, HN, SP, H, W)
        acc = acc + patch * wgt[:, :, k][:, :, None]
    return acc.reshape(B, COUT, H, W)

@@ -1,0 +1,302 @@
+from contextlib import ExitStack
+
+import concourse.mybir as mybir
+from concourse.masks import make_identity
+
+F32 = mybir.dt.float32
+BF16 = mybir.dt.bfloat16
+U32 = mybir.dt.uint32
+U8 = mybir.dt.uint8
+FP8X4 = mybir.dt.float8_e4m3fn_x4
+ALU = mybir.AluOpType
+ACTF = mybir.ActivationFunctionType
+AX = mybir.AxisListType
+
+P = 128
+NB = 4
+CIN = 512
+HH = 32
+COUT = 1024
+KW = 7
+KK = KW * KW
+ROWS = 4
+NCHUNK = HH // ROWS
+HALF = 512
+JP = HH + 6
+
+FLOPS = 2 * NB * COUT * CIN * HH * HH + 2 * NB * COUT * HH * HH * KK
+
+
+def reflect(u):
+    if u < 0:
+        return -u
+    if u > HH - 1:
+        return 2 * (HH - 1) - u
+    return u
+
+
+def tile_sam_pb_t_kernel(tc, logits, x, w3c, b3c, out):
+    nc = tc.nc
+    with ExitStack() as ctx:
+        ctx.enter_context(tc.manual_schedule())
+        const = ctx.enter_context(tc.tile_pool(name="const", bufs=1))
+        soft = ctx.enter_context(tc.tile_pool(name="soft", bufs=1))
+        wsp = ctx.enter_context(tc.tile_pool(name="wsp", bufs=2))
+        outp = ctx.enter_context(tc.tile_pool(name="outp", bufs=2))
+        psx = ctx.enter_context(tc.psum_pool(name="psx", bufs=2))
+        psacc = ctx.enter_context(tc.psum_pool(name="psacc", bufs=1))
+        pswt = ctx.enter_context(tc.psum_pool(name="pswt", bufs=2))
+
+        xq = const.tile([P, HH * P], U32, align_bytes=64)
+        xs = const.tile([P, HH * P], U8, align_bytes=64)
+        wq = const.tile([P, COUT], U32, align_bytes=64)
+        wsc = const.tile([P, COUT], U8, align_bytes=64)
+        perm = const.tile([P, 3 * P], F32)
+        ident_bf = const.tile([P, P], BF16)
+        bias_sb = const.tile([P, 8], F32)
+        w38 = const.tile([P, KK, JP, NB], F32)
+
+        lgs = []
+        wss = []
+        state = {}
+
+        def load_logits(ic):
+            lg = soft.tile([P, NB, KK, HH], BF16, name="lg")
+            for q in range(ROWS):
+                row = ROWS * ic + q
+                for b in range(NB):
+                    nc.sync.dma_start(
+                        out=lg[32 * q : 32 * q + 32, b],
+                        in_=logits[b, :, :, HH * row : HH * row + HH],
+                    )
+            lgs.append(lg)
+
+        def s1(ic, b):
+            if b == 0:
+                state["m"] = soft.tile([P, NB, HH], F32, name="mx")
+            nc.vector.tensor_reduce(
+                out=state["m"][:, b, :],
+                in_=lgs[ic][:, b].rearrange("p l j -> p j l"),
+                axis=AX.X,
+                op=ALU.max,
+            )
+
+        def s2(ic, eng):
+            state["e"] = soft.tile([P, NB, KK, HH], F32, name="ex")
+            eng.tensor_tensor(
+                out=state["e"][:],
+                in0=lgs[ic][:],
+                in1=state["m"][:].unsqueeze(2).to_broadcast([P, NB, KK, HH]),
+                op=ALU.subtract,
+            )
+            if ic + 1 < NCHUNK:
+                load_logits(ic + 1)
+
+        def s3(b):
+            nc.scalar.activation(out=state["e"][:, b], in_=state["e"][:, b], func=ACTF.Exp)
+
+        def s4(b):
+            if b == 0:
+                state["s"] = soft.tile([P, NB, HH], F32, name="sm")
+            nc.vector.tensor_reduce(
+                out=state["s"][:, b, :],
+                in_=state["e"][:, b].rearrange("p l j -> p j l"),
+                axis=AX.X,
+                op=ALU.add,
+            )
+
+        def s5():
+            state["r"] = soft.tile([P, NB, HH], F32, name="rs")
+            nc.vector.reciprocal(out=state["r"][:], in_=state["s"][:])
+
+        def s6(eng):
+            eng.tensor_tensor(
+                out=w38[:, :, 3 : 3 + HH, :],
+                in0=state["e"][:].rearrange("p b l j -> p l j b"),
+                in1=state["r"][:].rearrange("p b j -> p j b").unsqueeze(1).to_broadcast([P, KK, HH, NB]),
+                op=ALU.mult,
+            )
+            w5 = w38[:].rearrange("p (y d) j b -> p y d j b", d=KW)
+            pairs = []
+            for j in range(3):
+                for dx in range(3 - j):
+                    pairs.append((j, dx, 6 - 2 * j - dx))
+            for j in range(HH - 3, HH):
+                for dx in range(HH + 3 - j, KW):
+                    pairs.append((j, dx, 2 * HH + 4 - 2 * j - dx))
+            for j, dx, dxp in pairs:
+                eng.tensor_tensor(
+                    out=w5[:, :, dxp, 3 + j, :],
+                    in0=w5[:, :, dxp, 3 + j, :],
+                    in1=w5[:, :, dx, 3 + j, :],
+                    op=ALU.add,
+                )
+
+        def s8(k):
+            if k == 0:
+                wss.append(wsp.tile([P, KK, P], F32, name="ws"))
+            ws = wss[-1]
+            w38f = w38[:].rearrange("p l j b -> p l (j b)")
+            l0 = 4 * k
+            n = min(4, KK - l0)
+            wt = pswt.tile([P, 4, P], F32, name="wt")
+            for r in range(n):
+                st = NB * (6 - (l0 + r) % KW)
+                nc.tensor.transpose(wt[:, r, :], w38f[:, l0 + r, st : st + P], perm[:, P : 2 * P])
+            nc.scalar.copy(out=ws[:, l0 : l0 + n, :], in_=wt[:, 0:n, :])
+
+        make_identity(nc, ident_bf[:])
+        make_identity(nc, perm[:, 0:P])
+        nc.gpsimd.memset(w38[:], 0.0)
+        nc.vector.tensor_copy(out=perm[:, P : 2 * P], in_=perm[:, 0:P])
+        nc.vector.tensor_copy(out=perm[:, 2 * P : 3 * P], in_=perm[:, 0:P])
+
+        load_logits(0)
+
+        with tc.tile_pool(name="stage", bufs=1) as stage:
+            w_sb = stage.tile([P, 8, CIN], BF16)
+            nc.scalar.dma_start(out=w_sb[:], in_=w3c.rearrange("(g p) c -> p g c", p=P))
+            b_rows = stage.tile([P, P], BF16)
+            nc.vector.memset(b_rows[:], 0.0)
+            nc.scalar.dma_start(out=b_rows[0:8, :], in_=b3c.rearrange("(g o) -> g o", g=8))
+            x_sb = stage.tile([P, 4, NB, HH * HH], BF16)
+            for b in range(NB):
+                nc.scalar.dma_start(out=x_sb[:, :, b, :], in_=x[b].rearrange("(t p) i j -> p t (i j)", p=P))
+
+            w_grp = stage.tile([P, 8, P, 4], BF16, align_bytes=64)
+            for g in range(8):
+                wtb = pswt.tile([P, 4, P], BF16, name="wt")
+                for t in range(4):
+                    nc.tensor.transpose(wtb[:, t, :], w_sb[:, g, P * t : P * t + P], ident_bf[:])
+                nc.scalar.copy(out=w_grp[:, g], in_=wtb[:].rearrange("p t o -> p o t"))
+            btp = pswt.tile([P, P], BF16, name="wt")
+            nc.tensor.transpose(btp[:], b_rows[:], ident_bf[:])
+
+            for b in range(NB):
+                s1(0, b)
+            s2(0, nc.vector)
+            for b in range(NB):
+                s3(b)
+
+            nc.vector.tensor_copy(out=bias_sb[:], in_=btp[:, 0:8])
+            nc.vector.quantize_mx(
+                out=wq[:].bitcast(FP8X4),
+                scales=wsc[:],
+                in_=w_grp[:].rearrange("p g o t -> p (g o t)"),
+            )
+
+            for ch in range(4):
+                xg = stage.tile([P, 256, NB, 4], BF16, align_bytes=64, name="xg", bufs=2)
+                for b in range(NB):
+                    nc.vector.tensor_copy(
+                        out=xg[:, :, b, :],
+                        in_=x_sb[:, :, b, 256 * ch : 256 * ch + 256].rearrange("p t n -> p n t"),
+                    )
+                nc.vector.quantize_mx(
+                    out=xq[:, 1024 * ch : 1024 * ch + 1024].bitcast(FP8X4),
+                    scales=xs[:, 1024 * ch : 1024 * ch + 1024],
+                    in_=xg[:].rearrange("p n b t -> p (n b t)"),
+                )
+
+            for b in range(NB):
+                s4(b)
+            s5()
+            s6(nc.vector)
+            for k in range(13):
+                s8(k)
+
+        qp = ctx.enter_context(tc.tile_pool(name="qp", bufs=4))
+
+        units = []
+        for ic in range(NCHUNK):
+            for half in range(2):
+                for q in range(ROWS):
+                    for dy in range(KW):
+                        units.append((ic, half, q, dy))
+        xts = []
+
+        def emit_mx(u):
+            ic, half, q, dy = units[u]
+            a = reflect(ROWS * ic + q + dy - 3)
+            xt = psx.tile([P, HALF], F32, name="xt")
+            nc.tensor.matmul_mx(
+                out=xt[:],
+                lhsT=xq[:, P * a : P * a + P].bitcast(FP8X4),
+                lhsT_scale=xs[:, P * a : P * a + P],
+                rhs=wq[:, HALF * half : HALF * half + HALF].bitcast(FP8X4),
+                rhs_scale=wsc[:, HALF * half : HALF * half + HALF],
+                start=True,
+                stop=True,
+            )
+            xts.append(xt)
+
+        def prep_steps(ic):
+            steps = {}
+            for b in range(NB):
+                steps[1 + b] = (lambda bb: (lambda: s1(ic, bb)))(b)
+                steps[12 + b] = (lambda bb: (lambda: s3(bb)))(b)
+                steps[18 + b] = (lambda bb: (lambda: s4(bb)))(b)
+            steps[5] = lambda: s2(ic, nc.gpsimd)
+            steps[22] = s5
+            steps[23] = lambda: s6(nc.gpsimd)
+            for k in range(13):
+                steps[32 + k] = (lambda kk: (lambda: s8(kk)))(k)
+            return steps
+
+        emit_mx(0)
+        accs = []
+        osb = None
+        steps = {}
+        for u in range(len(units)):
+            ic, half, q, dy = units[u]
+            kidx = u % (2 * ROWS * KW)
+            if kidx == 0:
+                steps = prep_steps(ic + 1) if ic + 1 < NCHUNK else {}
+            if u + 1 < len(units):
+                emit_mx(u + 1)
+            ws = wss[ic]
+            qt = qp.tile([P, KW, HALF], F32, name="qt")
+            h0 = 32 * q + 16 * half
+            nc.vector.tensor_tensor(
+                out=qt[:].rearrange("p d (h c) -> p d h c", c=32),
+                in0=xts[u][:].rearrange("p (h c) -> p h c", c=32).unsqueeze(1).to_broadcast([P, KW, 16, 32]),
+                in1=ws[:, KW * dy : KW * dy + KW, h0 : h0 + 16].unsqueeze(3).to_broadcast([P, KW, 16, 32]),
+                op=ALU.mult,
+            )
+            if dy == 0:
+                accs = []
+                for g in range(4):
+                    accs.append(psacc.tile([P, P], F32, name="acc%d" % g))
+            for g in range(4):
+                for dx in range(KW):
+                    nc.tensor.matmul(
+                        out=accs[g][:],
+                        lhsT=qt[:, dx, P * g : P * g + P],
+                        rhs=perm[:, P - 12 + NB * dx : 2 * P - 12 + NB * dx],
+                        start=(dy == 0 and dx == 0),
+                        stop=(dy == KW - 1 and dx == KW - 1),
+                        is_transpose=True,
+                    )
+            if dy == KW - 1:
+                if q == 0:
+                    osb = outp.tile([P, 4, NB, ROWS, HH], F32, name="osb")
+                for g in range(4):
+                    gg = 4 * half + g
+                    nc.scalar.activation(
+                        out=osb[:, g, :, q, :],
+                        in_=accs[g][:].rearrange("o (j b) -> o b j", b=NB),
+                        func=ACTF.Identity,
+                        bias=bias_sb[:, gg : gg + 1],
+                        scale=1.0,
+                    )
+                if q == ROWS - 1:
+                    for g in range(4):
+                        gg = 4 * half + g
+                        nc.sync.dma_start(
+                            out=out[:, P * gg : P * gg + P, ROWS * ic : ROWS * ic + ROWS, :].rearrange(
+                                "b o q j -> o b (q j)"
+                            ),
+                            in_=osb[:, g].rearrange("o b q j -> o b (q j)"),
+                        )
+            if kidx in steps:
+                steps[kidx]()

@@ -23,6 +23,9 @@ ROWS = 4
 NCHUNK = HH // ROWS
 HALF = 512
 JP = HH + 6
+DXV = 5
+SLOTS = 2 * ROWS * KW
+KICK = 3
 
 FLOPS = 2 * NB * COUT * CIN * HH * HH + 2 * NB * COUT * HH * HH * KK
 
@@ -43,9 +46,10 @@ def tile_sam_pb_t_kernel(tc, logits, x, w3c, b3c, out):
         soft = ctx.enter_context(tc.tile_pool(name="soft", bufs=1))
         wsp = ctx.enter_context(tc.tile_pool(name="wsp", bufs=2))
         outp = ctx.enter_context(tc.tile_pool(name="outp", bufs=2))
-        psx = ctx.enter_context(tc.psum_pool(name="psx", bufs=2))
+        psa = ctx.enter_context(tc.psum_pool(name="psa", bufs=2))
+        psb = ctx.enter_context(tc.psum_pool(name="psb", bufs=1))
         psacc = ctx.enter_context(tc.psum_pool(name="psacc", bufs=1))
-        pswt = ctx.enter_context(tc.psum_pool(name="pswt", bufs=2))
+        pswt = ctx.enter_context(tc.psum_pool(name="pswt", bufs=1))
 
         xq = const.tile([P, HH * P], U32, align_bytes=64)
         xs = const.tile([P, HH * P], U8, align_bytes=64)
@@ -71,51 +75,7 @@ def tile_sam_pb_t_kernel(tc, logits, x, w3c, b3c, out):
                     )
             lgs.append(lg)
 
-        def s1(ic, b):
-            if b == 0:
-                state["m"] = soft.tile([P, NB, HH], F32, name="mx")
-            nc.vector.tensor_reduce(
-                out=state["m"][:, b, :],
-                in_=lgs[ic][:, b].rearrange("p l j -> p j l"),
-                axis=AX.X,
-                op=ALU.max,
-            )
-
-        def s2(ic, eng):
-            state["e"] = soft.tile([P, NB, KK, HH], F32, name="ex")
-            eng.tensor_tensor(
-                out=state["e"][:],
-                in0=lgs[ic][:],
-                in1=state["m"][:].unsqueeze(2).to_broadcast([P, NB, KK, HH]),
-                op=ALU.subtract,
-            )
-            if ic + 1 < NCHUNK:
-                load_logits(ic + 1)
-
-        def s3(b):
-            nc.scalar.activation(out=state["e"][:, b], in_=state["e"][:, b], func=ACTF.Exp)
-
-        def s4(b):
-            if b == 0:
-                state["s"] = soft.tile([P, NB, HH], F32, name="sm")
-            nc.vector.tensor_reduce(
-                out=state["s"][:, b, :],
-                in_=state["e"][:, b].rearrange("p l j -> p j l"),
-                axis=AX.X,
-                op=ALU.add,
-            )
-
-        def s5():
-            state["r"] = soft.tile([P, NB, HH], F32, name="rs")
-            nc.vector.reciprocal(out=state["r"][:], in_=state["s"][:])
-
-        def s6(eng):
-            eng.tensor_tensor(
-                out=w38[:, :, 3 : 3 + HH, :],
-                in0=state["e"][:].rearrange("p b l j -> p l j b"),
-                in1=state["r"][:].rearrange("p b j -> p j b").unsqueeze(1).to_broadcast([P, KK, HH, NB]),
-                op=ALU.mult,
-            )
+        def fold():
             w5 = w38[:].rearrange("p (y d) j b -> p y d j b", d=KW)
             pairs = []
             for j in range(3):
@@ -125,14 +85,14 @@ def tile_sam_pb_t_kernel(tc, logits, x, w3c, b3c, out):
                 for dx in range(HH + 3 - j, KW):
                     pairs.append((j, dx, 2 * HH + 4 - 2 * j - dx))
             for j, dx, dxp in pairs:
-                eng.tensor_tensor(
+                nc.vector.tensor_tensor(
                     out=w5[:, :, dxp, 3 + j, :],
                     in0=w5[:, :, dxp, 3 + j, :],
                     in1=w5[:, :, dx, 3 + j, :],
                     op=ALU.add,
                 )
 
-        def s8(k):
+        def turn(k):
             if k == 0:
                 wss.append(wsp.tile([P, KK, P], F32, name="ws"))
             ws = wss[-1]
@@ -144,6 +104,53 @@ def tile_sam_pb_t_kernel(tc, logits, x, w3c, b3c, out):
                 st = NB * (6 - (l0 + r) % KW)
                 nc.tensor.transpose(wt[:, r, :], w38f[:, l0 + r, st : st + P], perm[:, P : 2 * P])
             nc.scalar.copy(out=ws[:, l0 : l0 + n, :], in_=wt[:, 0:n, :])
+
+        def prepare(ic, k):
+            if k < 4:
+                if k == 0:
+                    state["m"] = soft.tile([P, NB, HH], F32, name="mx")
+                nc.vector.tensor_reduce(
+                    out=state["m"][:, k, :],
+                    in_=lgs[ic][:, k].rearrange("p l j -> p j l"),
+                    axis=AX.X,
+                    op=ALU.max,
+                )
+            elif k == 4:
+                state["n"] = soft.tile([P, NB, HH], F32, name="ng")
+                nc.vector.tensor_scalar_mul(out=state["n"][:], in0=state["m"][:], scalar1=-1.0)
+                state["e"] = soft.tile([P, NB, HH, KK], F32, name="ex")
+                state["s"] = soft.tile([P, NB, HH], F32, name="sm")
+            elif k < 21:
+                for col in range(8 * (k - 5), 8 * (k - 5) + 8):
+                    b = col // HH
+                    j = col % HH
+                    nc.scalar.activation(
+                        out=state["e"][:, b, j, :],
+                        in_=lgs[ic][:, b, :, j],
+                        func=ACTF.Exp,
+                        bias=state["n"][:, b, j : j + 1],
+                        scale=1.0,
+                        accum_out=state["s"][:, b, j : j + 1],
+                    )
+            elif k == 21:
+                state["r"] = soft.tile([P, NB, HH], F32, name="rs")
+                nc.vector.reciprocal(out=state["r"][:], in_=state["s"][:])
+                if ic + 1 < NCHUNK:
+                    load_logits(ic + 1)
+            elif k < 36:
+                if k % 2 == 0:
+                    dy = (k - 22) // 2
+                    eng = nc.vector if ic == 0 else nc.gpsimd
+                    eng.tensor_tensor(
+                        out=w38[:, KW * dy : KW * dy + KW, 3 : 3 + HH, :],
+                        in0=state["e"][:, :, :, KW * dy : KW * dy + KW].rearrange("p b j l -> p l j b"),
+                        in1=state["r"][:].rearrange("p b j -> p j b").unsqueeze(1).to_broadcast([P, KW, HH, NB]),
+                        op=ALU.mult,
+                    )
+            elif k == 37:
+                fold()
+            elif 38 <= k < 51:
+                turn(k - 38)
 
         make_identity(nc, ident_bf[:])
         make_identity(nc, perm[:, 0:P])
@@ -172,11 +179,8 @@ def tile_sam_pb_t_kernel(tc, logits, x, w3c, b3c, out):
             btp = pswt.tile([P, P], BF16, name="wt")
             nc.tensor.transpose(btp[:], b_rows[:], ident_bf[:])
 
-            for b in range(NB):
-                s1(0, b)
-            s2(0, nc.vector)
-            for b in range(NB):
-                s3(b)
+            for k in range(21):
+                prepare(0, k)
 
             nc.vector.tensor_copy(out=bias_sb[:], in_=btp[:, 0:8])
             nc.vector.quantize_mx(
@@ -198,14 +202,12 @@ def tile_sam_pb_t_kernel(tc, logits, x, w3c, b3c, out):
                     in_=xg[:].rearrange("p n b t -> p (n b t)"),
                 )
 
-            for b in range(NB):
-                s4(b)
-            s5()
-            s6(nc.vector)
-            for k in range(13):
-                s8(k)
+            for k in range(21, SLOTS):
+                prepare(0, k)
 
-        qp = ctx.enter_context(tc.tile_pool(name="qp", bufs=4))
+        qvp = ctx.enter_context(tc.tile_pool(name="qvp", bufs=3))
+        qgp = ctx.enter_context(tc.tile_pool(name="qgp", bufs=4))
+        xcp = ctx.enter_context(tc.tile_pool(name="xcp", bufs=2))
 
         units = []
         for ic in range(NCHUNK):
@@ -213,70 +215,85 @@ def tile_sam_pb_t_kernel(tc, logits, x, w3c, b3c, out):
                 for q in range(ROWS):
                     for dy in range(KW):
                         units.append((ic, half, q, dy))
-        xts = []
+        nu = len(units)
+        xas = []
+        qvs = []
+        qgs = []
 
-        def emit_mx(u):
+        def x_pass(u, pool, name, reps):
             ic, half, q, dy = units[u]
             a = reflect(ROWS * ic + q + dy - 3)
-            xt = psx.tile([P, HALF], F32, name="xt")
-            nc.tensor.matmul_mx(
-                out=xt[:],
-                lhsT=xq[:, P * a : P * a + P].bitcast(FP8X4),
-                lhsT_scale=xs[:, P * a : P * a + P],
-                rhs=wq[:, HALF * half : HALF * half + HALF].bitcast(FP8X4),
-                rhs_scale=wsc[:, HALF * half : HALF * half + HALF],
-                start=True,
-                stop=True,
-            )
-            xts.append(xt)
+            xt = pool.tile([P, HALF], F32, name=name)
+            for r in range(reps):
+                nc.tensor.matmul_mx(
+                    out=xt[:],
+                    lhsT=xq[:, P * a : P * a + P].bitcast(FP8X4),
+                    lhsT_scale=xs[:, P * a : P * a + P],
+                    rhs=wq[:, HALF * half : HALF * half + HALF].bitcast(FP8X4),
+                    rhs_scale=wsc[:, HALF * half : HALF * half + HALF],
+                    start=True,
+                    stop=True,
+                )
+            return xt
 
-        def prep_steps(ic):
-            steps = {}
-            for b in range(NB):
-                steps[1 + b] = (lambda bb: (lambda: s1(ic, bb)))(b)
-                steps[12 + b] = (lambda bb: (lambda: s3(bb)))(b)
-                steps[18 + b] = (lambda bb: (lambda: s4(bb)))(b)
-            steps[5] = lambda: s2(ic, nc.gpsimd)
-            steps[22] = s5
-            steps[23] = lambda: s6(nc.gpsimd)
-            for k in range(13):
-                steps[32 + k] = (lambda kk: (lambda: s8(kk)))(k)
-            return steps
-
-        emit_mx(0)
-        accs = []
-        osb = None
-        steps = {}
-        for u in range(len(units)):
+        def products(eng, u, xt, pool, name, d0, nd):
             ic, half, q, dy = units[u]
-            kidx = u % (2 * ROWS * KW)
-            if kidx == 0:
-                steps = prep_steps(ic + 1) if ic + 1 < NCHUNK else {}
-            if u + 1 < len(units):
-                emit_mx(u + 1)
-            ws = wss[ic]
-            qt = qp.tile([P, KW, HALF], F32, name="qt")
             h0 = 32 * q + 16 * half
-            nc.vector.tensor_tensor(
+            qt = pool.tile([P, nd, HALF], F32, name=name)
+            eng.tensor_tensor(
                 out=qt[:].rearrange("p d (h c) -> p d h c", c=32),
-                in0=xts[u][:].rearrange("p (h c) -> p h c", c=32).unsqueeze(1).to_broadcast([P, KW, 16, 32]),
-                in1=ws[:, KW * dy : KW * dy + KW, h0 : h0 + 16].unsqueeze(3).to_broadcast([P, KW, 16, 32]),
+                in0=xt[:].rearrange("p (h c) -> p h c", c=32).unsqueeze(1).to_broadcast([P, nd, 16, 32]),
+                in1=wss[ic][:, KW * dy + d0 : KW * dy + d0 + nd, h0 : h0 + 16]
+                .unsqueeze(3)
+                .to_broadcast([P, nd, 16, 32]),
                 op=ALU.mult,
             )
-            if dy == 0:
-                accs = []
-                for g in range(4):
-                    accs.append(psacc.tile([P, P], F32, name="acc%d" % g))
-            for g in range(4):
+            return qt
+
+        def vector_part(u):
+            qvs.append(products(nc.vector, u, xas[u], qvp, "qv", 0, DXV))
+
+        def gpsimd_part(u):
+            xb = x_pass(u, psb, "xb", 1)
+            xc = xcp.tile([P, HALF], F32, name="xc")
+            nc.scalar.copy(out=xc[:], in_=xb[:])
+            qgs.append(products(nc.gpsimd, u, xc, qgp, "qg", DXV, KW - DXV))
+
+        def gather(u, accs, g0):
+            dy = units[u][3]
+            for g in range(g0, g0 + 2):
                 for dx in range(KW):
+                    src = qvs[u][:, dx, P * g : P * g + P] if dx < DXV else qgs[u][:, dx - DXV, P * g : P * g + P]
                     nc.tensor.matmul(
                         out=accs[g][:],
-                        lhsT=qt[:, dx, P * g : P * g + P],
+                        lhsT=src,
                         rhs=perm[:, P - 12 + NB * dx : 2 * P - 12 + NB * dx],
                         start=(dy == 0 and dx == 0),
                         stop=(dy == KW - 1 and dx == KW - 1),
                         is_transpose=True,
                     )
+
+        xas.append(x_pass(0, psa, "xa", 1))
+        xas.append(x_pass(1, psa, "xa", 1))
+        for v in range(3):
+            gpsimd_part(v)
+        vector_part(0)
+        accs = []
+        osb = None
+        for u in range(nu):
+            ic, half, q, dy = units[u]
+            if u + 2 < nu:
+                xas.append(x_pass(u + 2, psa, "xa", KICK if dy == 0 else 1))
+            if u + 1 < nu:
+                vector_part(u + 1)
+            if dy == 0:
+                accs = []
+                for g in range(4):
+                    accs.append(psacc.tile([P, P], F32, name="acc%d" % g))
+            gather(u, accs, 0)
+            if u + 3 < nu:
+                gpsimd_part(u + 3)
+            gather(u, accs, 2)
             if dy == KW - 1:
                 if q == 0:
                     osb = outp.tile([P, 4, NB, ROWS, HH], F32, name="osb")
@@ -298,5 +315,5 @@ def tile_sam_pb_t_kernel(tc, logits, x, w3c, b3c, out):
                             ),
                             in_=osb[:, g].rearrange("o b q j -> o b (q j)"),
                         )
-            if kidx in steps:
-                steps[kidx]()
+            if ic + 1 < NCHUNK:
+                prepare(ic + 1, u % SLOTS)

@@ -25,7 +25,6 @@ HALF = 512
 JP = HH + 6
 DXV = 5
 SLOTS = 2 * ROWS * KW
-KICK = 3
 
 FLOPS = 2 * NB * COUT * CIN * HH * HH + 2 * NB * COUT * HH * HH * KK
 
@@ -106,22 +105,24 @@ def tile_sam_pb_t_kernel(tc, logits, x, w3c, b3c, out):
             nc.scalar.copy(out=ws[:, l0 : l0 + n, :], in_=wt[:, 0:n, :])
 
         def prepare(ic, k):
-            if k < 4:
+            if k < 8:
                 if k == 0:
                     state["m"] = soft.tile([P, NB, HH], F32, name="mx")
+                b = k // 2
+                j0 = 16 * (k % 2)
                 nc.vector.tensor_reduce(
-                    out=state["m"][:, k, :],
-                    in_=lgs[ic][:, k].rearrange("p l j -> p j l"),
+                    out=state["m"][:, b, j0 : j0 + 16],
+                    in_=lgs[ic][:, b, :, j0 : j0 + 16].rearrange("p l j -> p j l"),
                     axis=AX.X,
                     op=ALU.max,
                 )
-            elif k == 4:
+            elif k == 8:
                 state["n"] = soft.tile([P, NB, HH], F32, name="ng")
                 nc.vector.tensor_scalar_mul(out=state["n"][:], in0=state["m"][:], scalar1=-1.0)
                 state["e"] = soft.tile([P, NB, HH, KK], F32, name="ex")
                 state["s"] = soft.tile([P, NB, HH], F32, name="sm")
-            elif k < 21:
-                for col in range(8 * (k - 5), 8 * (k - 5) + 8):
+            elif k < 25:
+                for col in range(8 * (k - 9), 8 * (k - 9) + 8):
                     b = col // HH
                     j = col % HH
                     nc.scalar.activation(
@@ -132,14 +133,14 @@ def tile_sam_pb_t_kernel(tc, logits, x, w3c, b3c, out):
                         scale=1.0,
                         accum_out=state["s"][:, b, j : j + 1],
                     )
-            elif k == 21:
+            elif k == 25:
                 state["r"] = soft.tile([P, NB, HH], F32, name="rs")
                 nc.vector.reciprocal(out=state["r"][:], in_=state["s"][:])
                 if ic + 1 < NCHUNK:
                     load_logits(ic + 1)
-            elif k < 36:
+            elif k < 39:
                 if k % 2 == 0:
-                    dy = (k - 22) // 2
+                    dy = (k - 26) // 2
                     eng = nc.vector if ic == 0 else nc.gpsimd
                     eng.tensor_tensor(
                         out=w38[:, KW * dy : KW * dy + KW, 3 : 3 + HH, :],
@@ -147,10 +148,10 @@ def tile_sam_pb_t_kernel(tc, logits, x, w3c, b3c, out):
                         in1=state["r"][:].rearrange("p b j -> p j b").unsqueeze(1).to_broadcast([P, KW, HH, NB]),
                         op=ALU.mult,
                     )
-            elif k == 37:
+            elif k == 39:
                 fold()
-            elif 38 <= k < 51:
-                turn(k - 38)
+            elif k < 53:
+                turn(k - 40)
 
         make_identity(nc, ident_bf[:])
         make_identity(nc, perm[:, 0:P])
@@ -179,7 +180,7 @@ def tile_sam_pb_t_kernel(tc, logits, x, w3c, b3c, out):
             btp = pswt.tile([P, P], BF16, name="wt")
             nc.tensor.transpose(btp[:], b_rows[:], ident_bf[:])
 
-            for k in range(21):
+            for k in range(25):
                 prepare(0, k)
 
             nc.vector.tensor_copy(out=bias_sb[:], in_=btp[:, 0:8])
@@ -202,10 +203,10 @@ def tile_sam_pb_t_kernel(tc, logits, x, w3c, b3c, out):
                     in_=xg[:].rearrange("p n b t -> p (n b t)"),
                 )
 
-            for k in range(21, SLOTS):
+            for k in range(25, SLOTS):
                 prepare(0, k)
 
-        qvp = ctx.enter_context(tc.tile_pool(name="qvp", bufs=3))
+        qvp = ctx.enter_context(tc.tile_pool(name="qvp", bufs=4))
         qgp = ctx.enter_context(tc.tile_pool(name="qgp", bufs=4))
         xcp = ctx.enter_context(tc.tile_pool(name="xcp", bufs=2))
 
@@ -259,9 +260,9 @@ def tile_sam_pb_t_kernel(tc, logits, x, w3c, b3c, out):
             nc.scalar.copy(out=xc[:], in_=xb[:])
             qgs.append(products(nc.gpsimd, u, xc, qgp, "qg", DXV, KW - DXV))
 
-        def gather(u, accs, g0):
+        def gather(u, accs):
             dy = units[u][3]
-            for g in range(g0, g0 + 2):
+            for g in range(4):
                 for dx in range(KW):
                     src = qvs[u][:, dx, P * g : P * g + P] if dx < DXV else qgs[u][:, dx - DXV, P * g : P * g + P]
                     nc.tensor.matmul(
@@ -283,17 +284,16 @@ def tile_sam_pb_t_kernel(tc, logits, x, w3c, b3c, out):
         for u in range(nu):
             ic, half, q, dy = units[u]
             if u + 2 < nu:
-                xas.append(x_pass(u + 2, psa, "xa", KICK if dy == 0 else 1))
+                xas.append(x_pass(u + 2, psa, "xa", 2))
+            if u + 3 < nu:
+                gpsimd_part(u + 3)
             if u + 1 < nu:
                 vector_part(u + 1)
             if dy == 0:
                 accs = []
                 for g in range(4):
                     accs.append(psacc.tile([P, P], F32, name="acc%d" % g))
-            gather(u, accs, 0)
-            if u + 3 < nu:
-                gpsimd_part(u + 3)
-            gather(u, accs, 2)
+            gather(u, accs)
             if dy == KW - 1:
                 if q == 0:
                     osb = outp.tile([P, 4, NB, ROWS, HH], F32, name="osb")

@@ -23,7 +23,9 @@ ROWS = 4
 NCHUNK = HH // ROWS
 HALF = 512
 JP = HH + 6
-DXV = 5
+DX_SUM = 2
+DX_VEC = 2
+DX_GPS = 2
 SLOTS = 2 * ROWS * KW
 
 FLOPS = 2 * NB * COUT * CIN * HH * HH + 2 * NB * COUT * HH * HH * KK
@@ -206,8 +208,10 @@ def tile_sam_pb_t_kernel(tc, logits, x, w3c, b3c, out):
             for k in range(25, SLOTS):
                 prepare(0, k)
 
+        chp = ctx.enter_context(tc.tile_pool(name="chp", bufs=2))
         qvp = ctx.enter_context(tc.tile_pool(name="qvp", bufs=4))
         qgp = ctx.enter_context(tc.tile_pool(name="qgp", bufs=4))
+        qap = ctx.enter_context(tc.tile_pool(name="qap", bufs=4))
         xcp = ctx.enter_context(tc.tile_pool(name="xcp", bufs=2))
 
         units = []
@@ -218,14 +222,16 @@ def tile_sam_pb_t_kernel(tc, logits, x, w3c, b3c, out):
                         units.append((ic, half, q, dy))
         nu = len(units)
         xas = []
+        chs = []
         qvs = []
         qgs = []
+        qas = []
 
-        def x_pass(u, pool, name, reps):
+        def x_pass(u, pool, name):
             ic, half, q, dy = units[u]
             a = reflect(ROWS * ic + q + dy - 3)
             xt = pool.tile([P, HALF], F32, name=name)
-            for r in range(reps):
+            for r in range(2):
                 nc.tensor.matmul_mx(
                     out=xt[:],
                     lhsT=xq[:, P * a : P * a + P].bitcast(FP8X4),
@@ -237,10 +243,9 @@ def tile_sam_pb_t_kernel(tc, logits, x, w3c, b3c, out):
                 )
             return xt
 
-        def products(eng, u, xt, pool, name, d0, nd):
+        def products(eng, u, xt, qt, d0, nd):
             ic, half, q, dy = units[u]
             h0 = 32 * q + 16 * half
-            qt = pool.tile([P, nd, HALF], F32, name=name)
             eng.tensor_tensor(
                 out=qt[:].rearrange("p d (h c) -> p d h c", c=32),
                 in0=xt[:].rearrange("p (h c) -> p h c", c=32).unsqueeze(1).to_broadcast([P, nd, 16, 32]),
@@ -249,44 +254,87 @@ def tile_sam_pb_t_kernel(tc, logits, x, w3c, b3c, out):
                 .to_broadcast([P, nd, 16, 32]),
                 op=ALU.mult,
             )
-            return qt
 
         def vector_part(u):
-            qvs.append(products(nc.vector, u, xas[u], qvp, "qv", 0, DXV))
+            ic, half, q, dy = units[u]
+            h0 = 32 * q + 16 * half
+            qv = qvp.tile([P, DX_VEC, HALF], F32, name="qv")
+            products(nc.vector, u, xas[u], qv, DX_SUM, DX_VEC)
+            qvs.append(qv)
+            if dy == 0:
+                ch = chp.tile([P, DX_SUM, HALF], F32, name="ch")
+                products(nc.vector, u, xas[u], ch, 0, DX_SUM)
+                chs.append(ch)
+            else:
+                ch = chs[-1]
+                for d in range(DX_SUM):
+                    for h in range(16):
+                        nc.vector.scalar_tensor_tensor(
+                            out=ch[:, d, 32 * h : 32 * h + 32],
+                            in0=xas[u][:, 32 * h : 32 * h + 32],
+                            scalar=wss[ic][:, KW * dy + d, h0 + h : h0 + h + 1],
+                            in1=ch[:, d, 32 * h : 32 * h + 32],
+                            op0=ALU.mult,
+                            op1=ALU.add,
+                        )
 
-        def gpsimd_part(u):
-            xb = x_pass(u, psb, "xb", 1)
+        def side_part(u):
+            ic, half, q, dy = units[u]
+            h0 = 32 * q + 16 * half
+            xb = x_pass(u, psb, "xb")
             xc = xcp.tile([P, HALF], F32, name="xc")
             nc.scalar.copy(out=xc[:], in_=xb[:])
-            qgs.append(products(nc.gpsimd, u, xc, qgp, "qg", DXV, KW - DXV))
+            qg = qgp.tile([P, DX_GPS, HALF], F32, name="qg")
+            products(nc.gpsimd, u, xc, qg, DX_SUM + DX_VEC, DX_GPS)
+            qgs.append(qg)
+            qa = qap.tile([P, HALF], F32, name="qa")
+            for h in range(16):
+                nc.scalar.activation(
+                    out=qa[:, 32 * h : 32 * h + 32],
+                    in_=xb[:, 32 * h : 32 * h + 32],
+                    func=ACTF.Copy,
+                    scale=wss[ic][:, KW * dy + KW - 1, h0 + h : h0 + h + 1],
+                )
+            qas.append(qa)
 
         def gather(u, accs):
             dy = units[u][3]
+            cols = list(range(DX_SUM, KW))
+            if dy == KW - 1:
+                cols = cols + list(range(DX_SUM))
             for g in range(4):
-                for dx in range(KW):
-                    src = qvs[u][:, dx, P * g : P * g + P] if dx < DXV else qgs[u][:, dx - DXV, P * g : P * g + P]
+                og = slice(P * g, P * g + P)
+                for dx in cols:
+                    if dx < DX_SUM:
+                        src = chs[u // KW][:, dx, og]
+                    elif dx < DX_SUM + DX_VEC:
+                        src = qvs[u][:, dx - DX_SUM, og]
+                    elif dx < KW - 1:
+                        src = qgs[u][:, dx - DX_SUM - DX_VEC, og]
+                    else:
+                        src = qas[u][:, og]
                     nc.tensor.matmul(
                         out=accs[g][:],
                         lhsT=src,
                         rhs=perm[:, P - 12 + NB * dx : 2 * P - 12 + NB * dx],
-                        start=(dy == 0 and dx == 0),
-                        stop=(dy == KW - 1 and dx == KW - 1),
+                        start=(dy == 0 and dx == cols[0]),
+                        stop=(dy == KW - 1 and dx == cols[-1]),
                         is_transpose=True,
                     )
 
-        xas.append(x_pass(0, psa, "xa", 1))
-        xas.append(x_pass(1, psa, "xa", 1))
+        xas.append(x_pass(0, psa, "xa"))
+        xas.append(x_pass(1, psa, "xa"))
         for v in range(3):
-            gpsimd_part(v)
+            side_part(v)
         vector_part(0)
         accs = []
         osb = None
         for u in range(nu):
             ic, half, q, dy = units[u]
             if u + 2 < nu:
-                xas.append(x_pass(u + 2, psa, "xa", 2))
+                xas.append(x_pass(u + 2, psa, "xa"))
             if u + 3 < nu:
-                gpsimd_part(u + 3)
+                side_part(u + 3)
             if u + 1 < nu:
                 vector_part(u + 1)
             if dy == 0:

@@ -23,9 +23,8 @@ ROWS = 4
 NCHUNK = HH // ROWS
 HALF = 512
 JP = HH + 6
-DX_SUM = 2
-DX_VEC = 2
-DX_GPS = 2
+DX_VEC = 5
+DX_SCA = 2
 SLOTS = 2 * ROWS * KW
 
 FLOPS = 2 * NB * COUT * CIN * HH * HH + 2 * NB * COUT * HH * HH * KK
@@ -208,10 +207,9 @@ def tile_sam_pb_t_kernel(tc, logits, x, w3c, b3c, out):
             for k in range(25, SLOTS):
                 prepare(0, k)
 
-        chp = ctx.enter_context(tc.tile_pool(name="chp", bufs=2))
         qvp = ctx.enter_context(tc.tile_pool(name="qvp", bufs=4))
-        qgp = ctx.enter_context(tc.tile_pool(name="qgp", bufs=4))
-        qap = ctx.enter_context(tc.tile_pool(name="qap", bufs=4))
+        qap = ctx.enter_context(tc.tile_pool(name="qap", bufs=3))
+        csp = ctx.enter_context(tc.tile_pool(name="csp", bufs=2))
         xcp = ctx.enter_context(tc.tile_pool(name="xcp", bufs=2))
 
         units = []
@@ -222,10 +220,8 @@ def tile_sam_pb_t_kernel(tc, logits, x, w3c, b3c, out):
                         units.append((ic, half, q, dy))
         nu = len(units)
         xas = []
-        chs = []
         qvs = []
-        qgs = []
-        qas = []
+        css = []
 
         def x_pass(u, pool, name):
             ic, half, q, dy = units[u]
@@ -243,40 +239,19 @@ def tile_sam_pb_t_kernel(tc, logits, x, w3c, b3c, out):
                 )
             return xt
 
-        def products(eng, u, xt, qt, d0, nd):
-            ic, half, q, dy = units[u]
-            h0 = 32 * q + 16 * half
-            eng.tensor_tensor(
-                out=qt[:].rearrange("p d (h c) -> p d h c", c=32),
-                in0=xt[:].rearrange("p (h c) -> p h c", c=32).unsqueeze(1).to_broadcast([P, nd, 16, 32]),
-                in1=wss[ic][:, KW * dy + d0 : KW * dy + d0 + nd, h0 : h0 + 16]
-                .unsqueeze(3)
-                .to_broadcast([P, nd, 16, 32]),
-                op=ALU.mult,
-            )
-
         def vector_part(u):
             ic, half, q, dy = units[u]
             h0 = 32 * q + 16 * half
             qv = qvp.tile([P, DX_VEC, HALF], F32, name="qv")
-            products(nc.vector, u, xas[u], qv, DX_SUM, DX_VEC)
+            nc.vector.tensor_tensor(
+                out=qv[:].rearrange("p d (h c) -> p d h c", c=32),
+                in0=xas[u][:].rearrange("p (h c) -> p h c", c=32).unsqueeze(1).to_broadcast([P, DX_VEC, 16, 32]),
+                in1=wss[ic][:, KW * dy : KW * dy + DX_VEC, h0 : h0 + 16]
+                .unsqueeze(3)
+                .to_broadcast([P, DX_VEC, 16, 32]),
+                op=ALU.mult,
+            )
             qvs.append(qv)
-            if dy == 0:
-                ch = chp.tile([P, DX_SUM, HALF], F32, name="ch")
-                products(nc.vector, u, xas[u], ch, 0, DX_SUM)
-                chs.append(ch)
-            else:
-                ch = chs[-1]
-                for d in range(DX_SUM):
-                    for h in range(16):
-                        nc.vector.scalar_tensor_tensor(
-                            out=ch[:, d, 32 * h : 32 * h + 32],
-                            in0=xas[u][:, 32 * h : 32 * h + 32],
-                            scalar=wss[ic][:, KW * dy + d, h0 + h : h0 + h + 1],
-                            in1=ch[:, d, 32 * h : 32 * h + 32],
-                            op0=ALU.mult,
-                            op1=ALU.add,
-                        )
 
         def side_part(u):
             ic, half, q, dy = units[u]
@@ -284,41 +259,35 @@ def tile_sam_pb_t_kernel(tc, logits, x, w3c, b3c, out):
             xb = x_pass(u, psb, "xb")
             xc = xcp.tile([P, HALF], F32, name="xc")
             nc.scalar.copy(out=xc[:], in_=xb[:])
-            qg = qgp.tile([P, DX_GPS, HALF], F32, name="qg")
-            products(nc.gpsimd, u, xc, qg, DX_SUM + DX_VEC, DX_GPS)
-            qgs.append(qg)
-            qa = qap.tile([P, HALF], F32, name="qa")
-            for h in range(16):
-                nc.scalar.activation(
-                    out=qa[:, 32 * h : 32 * h + 32],
-                    in_=xb[:, 32 * h : 32 * h + 32],
-                    func=ACTF.Copy,
-                    scale=wss[ic][:, KW * dy + KW - 1, h0 + h : h0 + h + 1],
-                )
-            qas.append(qa)
+            if dy == 0:
+                qa = csp.tile([P, DX_SCA, HALF], F32, name="cs")
+                css.append(qa)
+            else:
+                qa = qap.tile([P, DX_SCA, HALF], F32, name="qa")
+            for d in range(DX_SCA):
+                for h in range(16):
+                    nc.scalar.activation(
+                        out=qa[:, d, 32 * h : 32 * h + 32],
+                        in_=xc[:, 32 * h : 32 * h + 32],
+                        func=ACTF.Copy,
+                        scale=wss[ic][:, KW * dy + DX_VEC + d, h0 + h : h0 + h + 1],
+                    )
+            if dy > 0:
+                nc.gpsimd.tensor_tensor(out=css[-1][:], in0=css[-1][:], in1=qa[:], op=ALU.add)
 
-        def gather(u, accs):
+        def gather(u, accs, g0):
             dy = units[u][3]
-            cols = list(range(DX_SUM, KW))
-            if dy == KW - 1:
-                cols = cols + list(range(DX_SUM))
-            for g in range(4):
+            last = dy == KW - 1
+            for g in range(g0, g0 + 2):
                 og = slice(P * g, P * g + P)
-                for dx in cols:
-                    if dx < DX_SUM:
-                        src = chs[u // KW][:, dx, og]
-                    elif dx < DX_SUM + DX_VEC:
-                        src = qvs[u][:, dx - DX_SUM, og]
-                    elif dx < KW - 1:
-                        src = qgs[u][:, dx - DX_SUM - DX_VEC, og]
-                    else:
-                        src = qas[u][:, og]
+                for dx in range(KW if last else DX_VEC):
+                    src = qvs[u][:, dx, og] if dx < DX_VEC else css[u // KW][:, dx - DX_VEC, og]
                     nc.tensor.matmul(
                         out=accs[g][:],
                         lhsT=src,
                         rhs=perm[:, P - 12 + NB * dx : 2 * P - 12 + NB * dx],
-                        start=(dy == 0 and dx == cols[0]),
-                        stop=(dy == KW - 1 and dx == cols[-1]),
+                        start=(dy == 0 and dx == 0),
+                        stop=(last and dx == KW - 1),
                         is_transpose=True,
                     )
 
@@ -333,15 +302,16 @@ def tile_sam_pb_t_kernel(tc, logits, x, w3c, b3c, out):
             ic, half, q, dy = units[u]
             if u + 2 < nu:
                 xas.append(x_pass(u + 2, psa, "xa"))
-            if u + 3 < nu:
-                side_part(u + 3)
             if u + 1 < nu:
                 vector_part(u + 1)
             if dy == 0:
                 accs = []
                 for g in range(4):
                     accs.append(psacc.tile([P, P], F32, name="acc%d" % g))
-            gather(u, accs)
+            gather(u, accs, 0)
+            if u + 3 < nu:
+                side_part(u + 3)
+            gather(u, accs, 2)
             if dy == KW - 1:
                 if q == 0:
                     osb = outp.tile([P, 4, NB, ROWS, HH], F32, name="osb")

@@ -24,7 +24,8 @@ NCHUNK = HH // ROWS
 HALF = 512
 JP = HH + 6
 DX_VEC = 5
-DX_SCA = 2
+DX_SCA = 5
+DX_GPS = 6
 SLOTS = 2 * ROWS * KW
 
 FLOPS = 2 * NB * COUT * CIN * HH * HH + 2 * NB * COUT * HH * HH * KK
@@ -92,14 +93,14 @@ def tile_sam_pb_t_kernel(tc, logits, x, w3c, b3c, out):
                     op=ALU.add,
                 )
 
-        def turn(k):
+        def turn(k, pool, name):
             if k == 0:
                 wss.append(wsp.tile([P, KK, P], F32, name="ws"))
             ws = wss[-1]
             w38f = w38[:].rearrange("p l j b -> p l (j b)")
             l0 = 4 * k
             n = min(4, KK - l0)
-            wt = pswt.tile([P, 4, P], F32, name="wt")
+            wt = pool.tile([P, 4, P], F32, name=name)
             for r in range(n):
                 st = NB * (6 - (l0 + r) % KW)
                 nc.tensor.transpose(wt[:, r, :], w38f[:, l0 + r, st : st + P], perm[:, P : 2 * P])
@@ -109,6 +110,9 @@ def tile_sam_pb_t_kernel(tc, logits, x, w3c, b3c, out):
             if k < 8:
                 if k == 0:
                     state["m"] = soft.tile([P, NB, HH], F32, name="mx")
+                    state["n"] = soft.tile([P, NB, HH], F32, name="ng")
+                    state["e"] = soft.tile([P, NB, HH, KK], F32, name="ex")
+                    state["s"] = soft.tile([P, NB, HH], F32, name="sm")
                 b = k // 2
                 j0 = 16 * (k % 2)
                 nc.vector.tensor_reduce(
@@ -117,13 +121,11 @@ def tile_sam_pb_t_kernel(tc, logits, x, w3c, b3c, out):
                     axis=AX.X,
                     op=ALU.max,
                 )
-            elif k == 8:
-                state["n"] = soft.tile([P, NB, HH], F32, name="ng")
-                nc.vector.tensor_scalar_mul(out=state["n"][:], in0=state["m"][:], scalar1=-1.0)
-                state["e"] = soft.tile([P, NB, HH, KK], F32, name="ex")
-                state["s"] = soft.tile([P, NB, HH], F32, name="sm")
-            elif k < 25:
-                for col in range(8 * (k - 9), 8 * (k - 9) + 8):
+                nc.vector.tensor_scalar_mul(
+                    out=state["n"][:, b, j0 : j0 + 16], in0=state["m"][:, b, j0 : j0 + 16], scalar1=-1.0
+                )
+            elif k < 24:
+                for col in range(8 * (k - 8), 8 * (k - 8) + 8):
                     b = col // HH
                     j = col % HH
                     nc.scalar.activation(
@@ -134,14 +136,14 @@ def tile_sam_pb_t_kernel(tc, logits, x, w3c, b3c, out):
                         scale=1.0,
                         accum_out=state["s"][:, b, j : j + 1],
                     )
-            elif k == 25:
+            elif k == 24:
                 state["r"] = soft.tile([P, NB, HH], F32, name="rs")
                 nc.vector.reciprocal(out=state["r"][:], in_=state["s"][:])
                 if ic + 1 < NCHUNK:
                     load_logits(ic + 1)
-            elif k < 39:
-                if k % 2 == 0:
-                    dy = (k - 26) // 2
+            elif k < 38:
+                if k % 2 == 1:
+                    dy = (k - 25) // 2
                     eng = nc.vector if ic == 0 else nc.gpsimd
                     eng.tensor_tensor(
                         out=w38[:, KW * dy : KW * dy + KW, 3 : 3 + HH, :],
@@ -149,10 +151,13 @@ def tile_sam_pb_t_kernel(tc, logits, x, w3c, b3c, out):
                         in1=state["r"][:].rearrange("p b j -> p j b").unsqueeze(1).to_broadcast([P, KW, HH, NB]),
                         op=ALU.mult,
                     )
-            elif k == 39:
+            elif k == 38:
                 fold()
-            elif k < 53:
-                turn(k - 40)
+            elif k < 52:
+                if ic == 0:
+                    turn(k - 39, psacc, "acc%d" % (k % 4))
+                else:
+                    turn(k - 39, pswt, "wt")
 
         make_identity(nc, ident_bf[:])
         make_identity(nc, perm[:, 0:P])
@@ -181,8 +186,10 @@ def tile_sam_pb_t_kernel(tc, logits, x, w3c, b3c, out):
             btp = pswt.tile([P, P], BF16, name="wt")
             nc.tensor.transpose(btp[:], b_rows[:], ident_bf[:])
 
-            for k in range(25):
+            for k in range(8):
                 prepare(0, k)
+                prepare(0, 8 + 2 * k)
+                prepare(0, 9 + 2 * k)
 
             nc.vector.tensor_copy(out=bias_sb[:], in_=btp[:, 0:8])
             nc.vector.quantize_mx(
@@ -204,11 +211,12 @@ def tile_sam_pb_t_kernel(tc, logits, x, w3c, b3c, out):
                     in_=xg[:].rearrange("p n b t -> p (n b t)"),
                 )
 
-            for k in range(25, SLOTS):
+            for k in range(24, SLOTS):
                 prepare(0, k)
 
         qvp = ctx.enter_context(tc.tile_pool(name="qvp", bufs=4))
-        qap = ctx.enter_context(tc.tile_pool(name="qap", bufs=3))
+        qap = ctx.enter_context(tc.tile_pool(name="qap", bufs=4))
+        pgp = ctx.enter_context(tc.tile_pool(name="pgp", bufs=2))
         csp = ctx.enter_context(tc.tile_pool(name="csp", bufs=2))
         xcp = ctx.enter_context(tc.tile_pool(name="xcp", bufs=2))
 
@@ -221,6 +229,7 @@ def tile_sam_pb_t_kernel(tc, logits, x, w3c, b3c, out):
         nu = len(units)
         xas = []
         qvs = []
+        qas = []
         css = []
 
         def x_pass(u, pool, name):
@@ -259,29 +268,41 @@ def tile_sam_pb_t_kernel(tc, logits, x, w3c, b3c, out):
             xb = x_pass(u, psb, "xb")
             xc = xcp.tile([P, HALF], F32, name="xc")
             nc.scalar.copy(out=xc[:], in_=xb[:])
+            qa = qap.tile([P, HALF], F32, name="qa")
+            for h in range(16):
+                nc.scalar.activation(
+                    out=qa[:, 32 * h : 32 * h + 32],
+                    in_=xc[:, 32 * h : 32 * h + 32],
+                    func=ACTF.Copy,
+                    scale=wss[ic][:, KW * dy + DX_SCA, h0 + h : h0 + h + 1],
+                )
+            qas.append(qa)
             if dy == 0:
-                qa = csp.tile([P, DX_SCA, HALF], F32, name="cs")
-                css.append(qa)
+                pg = csp.tile([P, HALF], F32, name="cs")
+                css.append(pg)
             else:
-                qa = qap.tile([P, DX_SCA, HALF], F32, name="qa")
-            for d in range(DX_SCA):
-                for h in range(16):
-                    nc.scalar.activation(
-                        out=qa[:, d, 32 * h : 32 * h + 32],
-                        in_=xc[:, 32 * h : 32 * h + 32],
-                        func=ACTF.Copy,
-                        scale=wss[ic][:, KW * dy + DX_VEC + d, h0 + h : h0 + h + 1],
-                    )
+                pg = pgp.tile([P, HALF], F32, name="pg")
+            nc.gpsimd.tensor_tensor(
+                out=pg[:].rearrange("p (h c) -> p h c", c=32),
+                in0=xc[:].rearrange("p (h c) -> p h c", c=32),
+                in1=wss[ic][:, KW * dy + DX_GPS, h0 : h0 + 16].unsqueeze(2).to_broadcast([P, 16, 32]),
+                op=ALU.mult,
+            )
             if dy > 0:
-                nc.gpsimd.tensor_tensor(out=css[-1][:], in0=css[-1][:], in1=qa[:], op=ALU.add)
+                nc.gpsimd.tensor_tensor(out=css[-1][:], in0=css[-1][:], in1=pg[:], op=ALU.add)
 
         def gather(u, accs, g0):
             dy = units[u][3]
             last = dy == KW - 1
             for g in range(g0, g0 + 2):
                 og = slice(P * g, P * g + P)
-                for dx in range(KW if last else DX_VEC):
-                    src = qvs[u][:, dx, og] if dx < DX_VEC else css[u // KW][:, dx - DX_VEC, og]
+                for dx in range(KW if last else DX_GPS):
+                    if dx < DX_VEC:
+                        src = qvs[u][:, dx, og]
+                    elif dx == DX_SCA:
+                        src = qas[u][:, og]
+                    else:
+                        src = css[u // KW][:, og]
                     nc.tensor.matmul(
                         out=accs[g][:],
                         lhsT=src,

@@ -24,8 +24,7 @@ NCHUNK = HH // ROWS
 HALF = 512
 JP = HH + 6
 DX_VEC = 5
-DX_SCA = 5
-DX_GPS = 6
+DX_SCA = 2
 SLOTS = 2 * ROWS * KW
 
 FLOPS = 2 * NB * COUT * CIN * HH * HH + 2 * NB * COUT * HH * HH * KK
@@ -215,8 +214,7 @@ def tile_sam_pb_t_kernel(tc, logits, x, w3c, b3c, out):
                 prepare(0, k)
 
         qvp = ctx.enter_context(tc.tile_pool(name="qvp", bufs=4))
-        qap = ctx.enter_context(tc.tile_pool(name="qap", bufs=4))
-        pgp = ctx.enter_context(tc.tile_pool(name="pgp", bufs=2))
+        qap = ctx.enter_context(tc.tile_pool(name="qap", bufs=3))
         csp = ctx.enter_context(tc.tile_pool(name="csp", bufs=2))
         xcp = ctx.enter_context(tc.tile_pool(name="xcp", bufs=2))
 
@@ -229,23 +227,21 @@ def tile_sam_pb_t_kernel(tc, logits, x, w3c, b3c, out):
         nu = len(units)
         xas = []
         qvs = []
-        qas = []
         css = []
 
         def x_pass(u, pool, name):
             ic, half, q, dy = units[u]
             a = reflect(ROWS * ic + q + dy - 3)
             xt = pool.tile([P, HALF], F32, name=name)
-            for r in range(2):
-                nc.tensor.matmul_mx(
-                    out=xt[:],
-                    lhsT=xq[:, P * a : P * a + P].bitcast(FP8X4),
-                    lhsT_scale=xs[:, P * a : P * a + P],
-                    rhs=wq[:, HALF * half : HALF * half + HALF].bitcast(FP8X4),
-                    rhs_scale=wsc[:, HALF * half : HALF * half + HALF],
-                    start=True,
-                    stop=True,
-                )
+            nc.tensor.matmul_mx(
+                out=xt[:],
+                lhsT=xq[:, P * a : P * a + P].bitcast(FP8X4),
+                lhsT_scale=xs[:, P * a : P * a + P],
+                rhs=wq[:, HALF * half : HALF * half + HALF].bitcast(FP8X4),
+                rhs_scale=wsc[:, HALF * half : HALF * half + HALF],
+                start=True,
+                stop=True,
+            )
             return xt
 
         def vector_part(u):
@@ -268,41 +264,29 @@ def tile_sam_pb_t_kernel(tc, logits, x, w3c, b3c, out):
             xb = x_pass(u, psb, "xb")
             xc = xcp.tile([P, HALF], F32, name="xc")
             nc.scalar.copy(out=xc[:], in_=xb[:])
-            qa = qap.tile([P, HALF], F32, name="qa")
-            for h in range(16):
-                nc.scalar.activation(
-                    out=qa[:, 32 * h : 32 * h + 32],
-                    in_=xc[:, 32 * h : 32 * h + 32],
-                    func=ACTF.Copy,
-                    scale=wss[ic][:, KW * dy + DX_SCA, h0 + h : h0 + h + 1],
-                )
-            qas.append(qa)
             if dy == 0:
-                pg = csp.tile([P, HALF], F32, name="cs")
-                css.append(pg)
+                qa = csp.tile([P, DX_SCA, HALF], F32, name="cs")
+                css.append(qa)
             else:
-                pg = pgp.tile([P, HALF], F32, name="pg")
-            nc.gpsimd.tensor_tensor(
-                out=pg[:].rearrange("p (h c) -> p h c", c=32),
-                in0=xc[:].rearrange("p (h c) -> p h c", c=32),
-                in1=wss[ic][:, KW * dy + DX_GPS, h0 : h0 + 16].unsqueeze(2).to_broadcast([P, 16, 32]),
-                op=ALU.mult,
-            )
+                qa = qap.tile([P, DX_SCA, HALF], F32, name="qa")
+            for d in range(DX_SCA):
+                for h in range(16):
+                    nc.scalar.activation(
+                        out=qa[:, d, 32 * h : 32 * h + 32],
+                        in_=xc[:, 32 * h : 32 * h + 32],
+                        func=ACTF.Copy,
+                        scale=wss[ic][:, KW * dy + DX_VEC + d, h0 + h : h0 + h + 1],
+                    )
             if dy > 0:
-                nc.gpsimd.tensor_tensor(out=css[-1][:], in0=css[-1][:], in1=pg[:], op=ALU.add)
+                nc.gpsimd.tensor_tensor(out=css[-1][:], in0=css[-1][:], in1=qa[:], op=ALU.add)
 
-        def gather(u, accs, g0):
+        def gather(u, accs):
             dy = units[u][3]
             last = dy == KW - 1
-            for g in range(g0, g0 + 2):
+            for g in range(4):
                 og = slice(P * g, P * g + P)
-                for dx in range(KW if last else DX_GPS):
-                    if dx < DX_VEC:
-                        src = qvs[u][:, dx, og]
-                    elif dx == DX_SCA:
-                        src = qas[u][:, og]
-                    else:
-                        src = css[u // KW][:, og]
+                for dx in range(KW if last else DX_VEC):
+                    src = qvs[u][:, dx, og] if dx < DX_VEC else css[u // KW][:, dx - DX_VEC, og]
                     nc.tensor.matmul(
                         out=accs[g][:],
                         lhsT=src,
@@ -323,16 +307,15 @@ def tile_sam_pb_t_kernel(tc, logits, x, w3c, b3c, out):
             ic, half, q, dy = units[u]
             if u + 2 < nu:
                 xas.append(x_pass(u + 2, psa, "xa"))
+            if u + 3 < nu:
+                side_part(u + 3)
             if u + 1 < nu:
                 vector_part(u + 1)
             if dy == 0:
                 accs = []
                 for g in range(4):
                     accs.append(psacc.tile([P, P], F32, name="acc%d" % g))
-            gather(u, accs, 0)
-            if u + 3 < nu:
-                side_part(u + 3)
-            gather(u, accs, 2)
+            gather(u, accs)
             if dy == KW - 1:
                 if q == 0:
                     osb = outp.tile([P, 4, NB, ROWS, HH], F32, name="osb")

@@ -15,26 +15,34 @@ AX = mybir.AxisListType
 P = 128
 NB = 4
 CIN = 512
-HH = 32
+PACK = 4
+SIDE = 32
 COUT = 1024
+SP = 32
+NHEAD = COUT // SP
 KW = 7
+PAD = KW // 2
 KK = KW * KW
-ROWS = 4
-NCHUNK = HH // ROWS
+ROWS = P // NHEAD
+NCHUNK = SIDE // ROWS
 HALF = 512
-JP = HH + 6
-DX_VEC = 5
-DX_SCA = 2
-SLOTS = 2 * ROWS * KW
+HEADS = HALF // SP
+NACC = HALF // P
+WIDE = SIDE + 2 * PAD
+UNITS = 2 * ROWS * KW
 
-FLOPS = 2 * NB * COUT * CIN * HH * HH + 2 * NB * COUT * HH * HH * KK
+DX_VEC = 5
+DX_SCA = KW - DX_VEC
+DY_SUM = 5
+
+FLOPS = 2 * NB * COUT * CIN * SIDE * SIDE + 2 * NB * COUT * SIDE * SIDE * KK
 
 
 def reflect(u):
     if u < 0:
         return -u
-    if u > HH - 1:
-        return 2 * (HH - 1) - u
+    if u > SIDE - 1:
+        return 2 * (SIDE - 1) - u
     return u
 
 
@@ -51,93 +59,90 @@ def tile_sam_pb_t_kernel(tc, logits, x, w3c, b3c, out):
         psacc = ctx.enter_context(tc.psum_pool(name="psacc", bufs=1))
         pswt = ctx.enter_context(tc.psum_pool(name="pswt", bufs=1))
 
-        xq = const.tile([P, HH * P], U32, align_bytes=64)
-        xs = const.tile([P, HH * P], U8, align_bytes=64)
+        xq = const.tile([P, SIDE * P], U32, align_bytes=64)
+        xs = const.tile([P, SIDE * P], U8, align_bytes=64)
         wq = const.tile([P, COUT], U32, align_bytes=64)
         wsc = const.tile([P, COUT], U8, align_bytes=64)
         perm = const.tile([P, 3 * P], F32)
         ident_bf = const.tile([P, P], BF16)
-        bias_sb = const.tile([P, 8], F32)
-        w38 = const.tile([P, KK, JP, NB], F32)
+        bias_sb = const.tile([P, COUT // P], F32)
+        wpad = const.tile([P, KK, WIDE, NB], F32)
 
-        lgs = []
-        wss = []
-        state = {}
+        logit_tiles = []
+        weight_tiles = []
+        cur = {}
 
         def load_logits(ic):
-            lg = soft.tile([P, NB, KK, HH], BF16, name="lg")
+            lg = soft.tile([P, NB, KK, SIDE], BF16, name="lg")
             for q in range(ROWS):
                 row = ROWS * ic + q
                 for b in range(NB):
                     nc.sync.dma_start(
-                        out=lg[32 * q : 32 * q + 32, b],
-                        in_=logits[b, :, :, HH * row : HH * row + HH],
+                        out=lg[NHEAD * q : NHEAD * q + NHEAD, b],
+                        in_=logits[b, :, :, SIDE * row : SIDE * row + SIDE],
                     )
-            lgs.append(lg)
+            logit_tiles.append(lg)
 
-        def fold():
-            w5 = w38[:].rearrange("p (y d) j b -> p y d j b", d=KW)
-            pairs = []
-            for j in range(3):
-                for dx in range(3 - j):
-                    pairs.append((j, dx, 6 - 2 * j - dx))
-            for j in range(HH - 3, HH):
-                for dx in range(HH + 3 - j, KW):
-                    pairs.append((j, dx, 2 * HH + 4 - 2 * j - dx))
-            for j, dx, dxp in pairs:
-                nc.vector.tensor_tensor(
-                    out=w5[:, :, dxp, 3 + j, :],
-                    in0=w5[:, :, dxp, 3 + j, :],
-                    in1=w5[:, :, dx, 3 + j, :],
-                    op=ALU.add,
-                )
+        def fold_mirrored_columns():
+            w5 = wpad[:].rearrange("p (y d) j b -> p y d j b", d=KW)
+            for j in list(range(PAD)) + list(range(SIDE - PAD, SIDE)):
+                for dx in range(KW):
+                    c = j + dx - PAD
+                    if c != reflect(c):
+                        dxm = reflect(c) - j + PAD
+                        nc.vector.tensor_tensor(
+                            out=w5[:, :, dxm, PAD + j, :],
+                            in0=w5[:, :, dxm, PAD + j, :],
+                            in1=w5[:, :, dx, PAD + j, :],
+                            op=ALU.add,
+                        )
 
-        def turn(k, pool, name):
+        def transpose_weights(k, pool, name):
             if k == 0:
-                wss.append(wsp.tile([P, KK, P], F32, name="ws"))
-            ws = wss[-1]
-            w38f = w38[:].rearrange("p l j b -> p l (j b)")
+                weight_tiles.append(wsp.tile([P, KK, P], F32, name="ws"))
+            ws = weight_tiles[-1]
+            flat = wpad[:].rearrange("p l j b -> p l (j b)")
             l0 = 4 * k
             n = min(4, KK - l0)
             wt = pool.tile([P, 4, P], F32, name=name)
             for r in range(n):
-                st = NB * (6 - (l0 + r) % KW)
-                nc.tensor.transpose(wt[:, r, :], w38f[:, l0 + r, st : st + P], perm[:, P : 2 * P])
+                first = NB * (2 * PAD - (l0 + r) % KW)
+                nc.tensor.transpose(wt[:, r, :], flat[:, l0 + r, first : first + P], perm[:, P : 2 * P])
             nc.scalar.copy(out=ws[:, l0 : l0 + n, :], in_=wt[:, 0:n, :])
 
         def prepare(ic, k):
             if k < 8:
                 if k == 0:
-                    state["m"] = soft.tile([P, NB, HH], F32, name="mx")
-                    state["n"] = soft.tile([P, NB, HH], F32, name="ng")
-                    state["e"] = soft.tile([P, NB, HH, KK], F32, name="ex")
-                    state["s"] = soft.tile([P, NB, HH], F32, name="sm")
+                    cur["max"] = soft.tile([P, NB, SIDE], F32, name="mx")
+                    cur["neg"] = soft.tile([P, NB, SIDE], F32, name="ng")
+                    cur["exp"] = soft.tile([P, NB, SIDE, KK], F32, name="ex")
+                    cur["sum"] = soft.tile([P, NB, SIDE], F32, name="sm")
                 b = k // 2
                 j0 = 16 * (k % 2)
                 nc.vector.tensor_reduce(
-                    out=state["m"][:, b, j0 : j0 + 16],
-                    in_=lgs[ic][:, b, :, j0 : j0 + 16].rearrange("p l j -> p j l"),
+                    out=cur["max"][:, b, j0 : j0 + 16],
+                    in_=logit_tiles[ic][:, b, :, j0 : j0 + 16].rearrange("p l j -> p j l"),
                     axis=AX.X,
                     op=ALU.max,
                 )
                 nc.vector.tensor_scalar_mul(
-                    out=state["n"][:, b, j0 : j0 + 16], in0=state["m"][:, b, j0 : j0 + 16], scalar1=-1.0
+                    out=cur["neg"][:, b, j0 : j0 + 16], in0=cur["max"][:, b, j0 : j0 + 16], scalar1=-1.0
                 )
             elif k < 24:
                 for col in range(8 * (k - 8), 8 * (k - 8) + 8):
-                    b = col // HH
-                    j = col % HH
+                    b = col // SIDE
+                    j = col % SIDE
                     nc.scalar.activation(
-                        out=state["e"][:, b, j, :],
-                        in_=lgs[ic][:, b, :, j],
+                        out=cur["exp"][:, b, j, :],
+                        in_=logit_tiles[ic][:, b, :, j],
                         func=ACTF.Exp,
-                        bias=state["n"][:, b, j : j + 1],
+                        bias=cur["neg"][:, b, j : j + 1],
                         scale=1.0,
-                        accum_out=state["s"][:, b, j : j + 1],
+                        accum_out=cur["sum"][:, b, j : j + 1],
                     )
             elif k == 24:
-                state["r"] = soft.tile([P, NB, HH], F32, name="rs")
-                nc.vector.reciprocal(out=state["r"][:], in_=state["s"][:])
+                cur["inv"] = soft.tile([P, NB, SIDE], F32, name="rs")
+                nc.vector.reciprocal(out=cur["inv"][:], in_=cur["sum"][:])
                 if ic + 1 < NCHUNK:
                     load_logits(ic + 1)
             elif k < 38:
@@ -145,41 +150,41 @@ def tile_sam_pb_t_kernel(tc, logits, x, w3c, b3c, out):
                     dy = (k - 25) // 2
                     eng = nc.vector if ic == 0 else nc.gpsimd
                     eng.tensor_tensor(
-                        out=w38[:, KW * dy : KW * dy + KW, 3 : 3 + HH, :],
-                        in0=state["e"][:, :, :, KW * dy : KW * dy + KW].rearrange("p b j l -> p l j b"),
-                        in1=state["r"][:].rearrange("p b j -> p j b").unsqueeze(1).to_broadcast([P, KW, HH, NB]),
+                        out=wpad[:, KW * dy : KW * dy + KW, PAD : PAD + SIDE, :],
+                        in0=cur["exp"][:, :, :, KW * dy : KW * dy + KW].rearrange("p b j l -> p l j b"),
+                        in1=cur["inv"][:].rearrange("p b j -> p j b").unsqueeze(1).to_broadcast([P, KW, SIDE, NB]),
                         op=ALU.mult,
                     )
             elif k == 38:
-                fold()
+                fold_mirrored_columns()
             elif k < 52:
                 if ic == 0:
-                    turn(k - 39, psacc, "acc%d" % (k % 4))
+                    transpose_weights(k - 39, psacc, "acc%d" % (k % NACC))
                 else:
-                    turn(k - 39, pswt, "wt")
+                    transpose_weights(k - 39, pswt, "wt")
 
         make_identity(nc, ident_bf[:])
         make_identity(nc, perm[:, 0:P])
-        nc.gpsimd.memset(w38[:], 0.0)
+        nc.gpsimd.memset(wpad[:], 0.0)
         nc.vector.tensor_copy(out=perm[:, P : 2 * P], in_=perm[:, 0:P])
         nc.vector.tensor_copy(out=perm[:, 2 * P : 3 * P], in_=perm[:, 0:P])
 
         load_logits(0)
 
         with tc.tile_pool(name="stage", bufs=1) as stage:
-            w_sb = stage.tile([P, 8, CIN], BF16)
+            w_sb = stage.tile([P, COUT // P, CIN], BF16)
             nc.scalar.dma_start(out=w_sb[:], in_=w3c.rearrange("(g p) c -> p g c", p=P))
             b_rows = stage.tile([P, P], BF16)
             nc.vector.memset(b_rows[:], 0.0)
-            nc.scalar.dma_start(out=b_rows[0:8, :], in_=b3c.rearrange("(g o) -> g o", g=8))
-            x_sb = stage.tile([P, 4, NB, HH * HH], BF16)
+            nc.scalar.dma_start(out=b_rows[0 : COUT // P, :], in_=b3c.rearrange("(g o) -> g o", g=COUT // P))
+            x_sb = stage.tile([P, PACK, NB, SIDE * SIDE], BF16)
             for b in range(NB):
                 nc.scalar.dma_start(out=x_sb[:, :, b, :], in_=x[b].rearrange("(t p) i j -> p t (i j)", p=P))
 
-            w_grp = stage.tile([P, 8, P, 4], BF16, align_bytes=64)
-            for g in range(8):
-                wtb = pswt.tile([P, 4, P], BF16, name="wt")
-                for t in range(4):
+            w_grp = stage.tile([P, COUT // P, P, PACK], BF16, align_bytes=64)
+            for g in range(COUT // P):
+                wtb = pswt.tile([P, PACK, P], BF16, name="wt")
+                for t in range(PACK):
                     nc.tensor.transpose(wtb[:, t, :], w_sb[:, g, P * t : P * t + P], ident_bf[:])
                 nc.scalar.copy(out=w_grp[:, g], in_=wtb[:].rearrange("p t o -> p o t"))
             btp = pswt.tile([P, P], BF16, name="wt")
@@ -190,27 +195,27 @@ def tile_sam_pb_t_kernel(tc, logits, x, w3c, b3c, out):
                 prepare(0, 8 + 2 * k)
                 prepare(0, 9 + 2 * k)
 
-            nc.vector.tensor_copy(out=bias_sb[:], in_=btp[:, 0:8])
+            nc.vector.tensor_copy(out=bias_sb[:], in_=btp[:, 0 : COUT // P])
             nc.vector.quantize_mx(
                 out=wq[:].bitcast(FP8X4),
                 scales=wsc[:],
                 in_=w_grp[:].rearrange("p g o t -> p (g o t)"),
             )
 
-            for ch in range(4):
-                xg = stage.tile([P, 256, NB, 4], BF16, align_bytes=64, name="xg", bufs=2)
+            for part in range(4):
+                xg = stage.tile([P, 256, NB, PACK], BF16, align_bytes=64, name="xg", bufs=2)
                 for b in range(NB):
                     nc.vector.tensor_copy(
                         out=xg[:, :, b, :],
-                        in_=x_sb[:, :, b, 256 * ch : 256 * ch + 256].rearrange("p t n -> p n t"),
+                        in_=x_sb[:, :, b, 256 * part : 256 * part + 256].rearrange("p t n -> p n t"),
                     )
                 nc.vector.quantize_mx(
-                    out=xq[:, 1024 * ch : 1024 * ch + 1024].bitcast(FP8X4),
-                    scales=xs[:, 1024 * ch : 1024 * ch + 1024],
+                    out=xq[:, 1024 * part : 1024 * part + 1024].bitcast(FP8X4),
+                    scales=xs[:, 1024 * part : 1024 * part + 1024],
                     in_=xg[:].rearrange("p n b t -> p (n b t)"),
                 )
 
-            for k in range(24, SLOTS):
+            for k in range(24, UNITS):
                 prepare(0, k)
 
         qvp = ctx.enter_context(tc.tile_pool(name="qvp", bufs=4))
@@ -225,13 +230,14 @@ def tile_sam_pb_t_kernel(tc, logits, x, w3c, b3c, out):
                     for dy in range(KW):
                         units.append((ic, half, q, dy))
         nu = len(units)
-        xas = []
-        qvs = []
-        css = []
+        x3_vector = []
+        prod_vector = []
+        prod_scalar = []
+        sums = []
 
-        def x_pass(u, pool, name):
+        def x3_pass(u, pool, name):
             ic, half, q, dy = units[u]
-            a = reflect(ROWS * ic + q + dy - 3)
+            a = reflect(ROWS * ic + q + dy - PAD)
             xt = pool.tile([P, HALF], F32, name=name)
             nc.tensor.matmul_mx(
                 out=xt[:],
@@ -246,81 +252,92 @@ def tile_sam_pb_t_kernel(tc, logits, x, w3c, b3c, out):
 
         def vector_part(u):
             ic, half, q, dy = units[u]
-            h0 = 32 * q + 16 * half
+            h0 = NHEAD * q + HEADS * half
             qv = qvp.tile([P, DX_VEC, HALF], F32, name="qv")
             nc.vector.tensor_tensor(
-                out=qv[:].rearrange("p d (h c) -> p d h c", c=32),
-                in0=xas[u][:].rearrange("p (h c) -> p h c", c=32).unsqueeze(1).to_broadcast([P, DX_VEC, 16, 32]),
-                in1=wss[ic][:, KW * dy : KW * dy + DX_VEC, h0 : h0 + 16]
+                out=qv[:].rearrange("p d (h c) -> p d h c", c=SP),
+                in0=x3_vector[u][:]
+                .rearrange("p (h c) -> p h c", c=SP)
+                .unsqueeze(1)
+                .to_broadcast([P, DX_VEC, HEADS, SP]),
+                in1=weight_tiles[ic][:, KW * dy : KW * dy + DX_VEC, h0 : h0 + HEADS]
                 .unsqueeze(3)
-                .to_broadcast([P, DX_VEC, 16, 32]),
+                .to_broadcast([P, DX_VEC, HEADS, SP]),
                 op=ALU.mult,
             )
-            qvs.append(qv)
+            prod_vector.append(qv)
 
-        def side_part(u):
+        def scalar_part(u):
             ic, half, q, dy = units[u]
-            h0 = 32 * q + 16 * half
-            xb = x_pass(u, psb, "xb")
+            h0 = NHEAD * q + HEADS * half
+            xb = x3_pass(u, psb, "xb")
             xc = xcp.tile([P, HALF], F32, name="xc")
             nc.scalar.copy(out=xc[:], in_=xb[:])
             if dy == 0:
                 qa = csp.tile([P, DX_SCA, HALF], F32, name="cs")
-                css.append(qa)
+                sums.append(qa)
             else:
                 qa = qap.tile([P, DX_SCA, HALF], F32, name="qa")
             for d in range(DX_SCA):
-                for h in range(16):
+                for h in range(HEADS):
                     nc.scalar.activation(
-                        out=qa[:, d, 32 * h : 32 * h + 32],
-                        in_=xc[:, 32 * h : 32 * h + 32],
+                        out=qa[:, d, SP * h : SP * h + SP],
+                        in_=xc[:, SP * h : SP * h + SP],
                         func=ACTF.Copy,
-                        scale=wss[ic][:, KW * dy + DX_VEC + d, h0 + h : h0 + h + 1],
+                        scale=weight_tiles[ic][:, KW * dy + DX_VEC + d, h0 + h : h0 + h + 1],
                     )
-            if dy > 0:
-                nc.gpsimd.tensor_tensor(out=css[-1][:], in0=css[-1][:], in1=qa[:], op=ALU.add)
+            if 0 < dy < DY_SUM:
+                nc.gpsimd.tensor_tensor(out=sums[-1][:], in0=sums[-1][:], in1=qa[:], op=ALU.add)
+            prod_scalar.append(qa)
 
-        def gather(u, accs):
+        def add_up(u, accs):
             dy = units[u][3]
-            last = dy == KW - 1
-            for g in range(4):
-                og = slice(P * g, P * g + P)
-                for dx in range(KW if last else DX_VEC):
-                    src = qvs[u][:, dx, og] if dx < DX_VEC else css[u // KW][:, dx - DX_VEC, og]
+            terms = []
+            for dx in range(DX_VEC):
+                terms.append((dx, prod_vector[u][:, dx, :]))
+            if dy >= DY_SUM:
+                for d in range(DX_SCA):
+                    terms.append((DX_VEC + d, prod_scalar[u][:, d, :]))
+            if dy == KW - 1:
+                for d in range(DX_SCA):
+                    terms.append((DX_VEC + d, sums[u // KW][:, d, :]))
+            for g in range(NACC):
+                for n, (dx, term) in enumerate(terms):
+                    shift = NB * (dx - PAD)
                     nc.tensor.matmul(
                         out=accs[g][:],
-                        lhsT=src,
-                        rhs=perm[:, P - 12 + NB * dx : 2 * P - 12 + NB * dx],
-                        start=(dy == 0 and dx == 0),
-                        stop=(last and dx == KW - 1),
+                        lhsT=term[:, P * g : P * g + P],
+                        rhs=perm[:, P + shift : 2 * P + shift],
+                        start=(dy == 0 and n == 0),
+                        stop=(dy == KW - 1 and n == len(terms) - 1),
                         is_transpose=True,
                     )
 
-        xas.append(x_pass(0, psa, "xa"))
-        xas.append(x_pass(1, psa, "xa"))
+        x3_vector.append(x3_pass(0, psa, "xa"))
+        x3_vector.append(x3_pass(1, psa, "xa"))
         for v in range(3):
-            side_part(v)
+            scalar_part(v)
         vector_part(0)
         accs = []
         osb = None
         for u in range(nu):
             ic, half, q, dy = units[u]
             if u + 2 < nu:
-                xas.append(x_pass(u + 2, psa, "xa"))
+                x3_vector.append(x3_pass(u + 2, psa, "xa"))
             if u + 3 < nu:
-                side_part(u + 3)
+                scalar_part(u + 3)
             if u + 1 < nu:
                 vector_part(u + 1)
             if dy == 0:
                 accs = []
-                for g in range(4):
+                for g in range(NACC):
                     accs.append(psacc.tile([P, P], F32, name="acc%d" % g))
-            gather(u, accs)
+            add_up(u, accs)
             if dy == KW - 1:
                 if q == 0:
-                    osb = outp.tile([P, 4, NB, ROWS, HH], F32, name="osb")
-                for g in range(4):
-                    gg = 4 * half + g
+                    osb = outp.tile([P, NACC, NB, ROWS, SIDE], F32, name="osb")
+                for g in range(NACC):
+                    gg = NACC * half + g
                     nc.scalar.activation(
                         out=osb[:, g, :, q, :],
                         in_=accs[g][:].rearrange("o (j b) -> o b j", b=NB),
@@ -329,8 +346,8 @@ def tile_sam_pb_t_kernel(tc, logits, x, w3c, b3c, out):
                         scale=1.0,
                     )
                 if q == ROWS - 1:
-                    for g in range(4):
-                        gg = 4 * half + g
+                    for g in range(NACC):
+                        gg = NACC * half + g
                         nc.sync.dma_start(
                             out=out[:, P * gg : P * gg + P, ROWS * ic : ROWS * ic + ROWS, :].rearrange(
                                 "b o q j -> o b (q j)"
@@ -338,4 +355,4 @@ def tile_sam_pb_t_kernel(tc, logits, x, w3c, b3c, out):
                             in_=osb[:, g].rearrange("o b q j -> o b (q j)"),
                         )
             if ic + 1 < NCHUNK:
-                prepare(ic + 1, u % SLOTS)
+                prepare(ic + 1, u % UNITS)

from contextlib import ExitStack

import concourse.mybir as mybir
from concourse.masks import make_identity

F32 = mybir.dt.float32
BF16 = mybir.dt.bfloat16
U32 = mybir.dt.uint32
U8 = mybir.dt.uint8
FP8X4 = mybir.dt.float8_e4m3fn_x4
ALU = mybir.AluOpType
ACTF = mybir.ActivationFunctionType
AX = mybir.AxisListType

P = 128
NB = 4
CIN = 512
PACK = 4
SIDE = 32
COUT = 1024
SP = 32
NHEAD = COUT // SP
KW = 7
PAD = KW // 2
KK = KW * KW
ROWS = P // NHEAD
NCHUNK = SIDE // ROWS
HALF = 512
HEADS = HALF // SP
NACC = HALF // P
WIDE = SIDE + 2 * PAD
UNITS = 2 * ROWS * KW

DX_VEC = 5
DX_SCA = KW - DX_VEC
DY_SUM = 5

FLOPS = 2 * NB * COUT * CIN * SIDE * SIDE + 2 * NB * COUT * SIDE * SIDE * KK


def reflect(u):
    if u < 0:
        return -u
    if u > SIDE - 1:
        return 2 * (SIDE - 1) - u
    return u


def tile_sam_pb_t_kernel(tc, logits, x, w3c, b3c, out):
    nc = tc.nc
    with ExitStack() as ctx:
        ctx.enter_context(tc.manual_schedule())
        const = ctx.enter_context(tc.tile_pool(name="const", bufs=1))
        soft = ctx.enter_context(tc.tile_pool(name="soft", bufs=1))
        wsp = ctx.enter_context(tc.tile_pool(name="wsp", bufs=2))
        outp = ctx.enter_context(tc.tile_pool(name="outp", bufs=2))
        psa = ctx.enter_context(tc.psum_pool(name="psa", bufs=2))
        psb = ctx.enter_context(tc.psum_pool(name="psb", bufs=1))
        psacc = ctx.enter_context(tc.psum_pool(name="psacc", bufs=1))
        pswt = ctx.enter_context(tc.psum_pool(name="pswt", bufs=1))

        xq = const.tile([P, SIDE * P], U32, align_bytes=64)
        xs = const.tile([P, SIDE * P], U8, align_bytes=64)
        wq = const.tile([P, COUT], U32, align_bytes=64)
        wsc = const.tile([P, COUT], U8, align_bytes=64)
        perm = const.tile([P, 3 * P], F32)
        ident_bf = const.tile([P, P], BF16)
        bias_sb = const.tile([P, COUT // P], F32)
        wpad = const.tile([P, KK, WIDE, NB], F32)

        logit_tiles = []
        weight_tiles = []
        cur = {}

        def load_logits(ic):
            lg = soft.tile([P, NB, KK, SIDE], BF16, name="lg")
            for q in range(ROWS):
                row = ROWS * ic + q
                for b in range(NB):
                    nc.sync.dma_start(
                        out=lg[NHEAD * q : NHEAD * q + NHEAD, b],
                        in_=logits[b, :, :, SIDE * row : SIDE * row + SIDE],
                    )
            logit_tiles.append(lg)

        def fold_mirrored_columns():
            w5 = wpad[:].rearrange("p (y d) j b -> p y d j b", d=KW)
            for j in list(range(PAD)) + list(range(SIDE - PAD, SIDE)):
                for dx in range(KW):
                    c = j + dx - PAD
                    if c != reflect(c):
                        dxm = reflect(c) - j + PAD
                        nc.vector.tensor_tensor(
                            out=w5[:, :, dxm, PAD + j, :],
                            in0=w5[:, :, dxm, PAD + j, :],
                            in1=w5[:, :, dx, PAD + j, :],
                            op=ALU.add,
                        )

        def transpose_weights(k, pool, name):
            if k == 0:
                weight_tiles.append(wsp.tile([P, KK, P], F32, name="ws"))
            ws = weight_tiles[-1]
            flat = wpad[:].rearrange("p l j b -> p l (j b)")
            l0 = 4 * k
            n = min(4, KK - l0)
            wt = pool.tile([P, 4, P], F32, name=name)
            for r in range(n):
                first = NB * (2 * PAD - (l0 + r) % KW)
                nc.tensor.transpose(wt[:, r, :], flat[:, l0 + r, first : first + P], perm[:, P : 2 * P])
            nc.scalar.copy(out=ws[:, l0 : l0 + n, :], in_=wt[:, 0:n, :])

        def prepare(ic, k):
            if k < 8:
                if k == 0:
                    cur["max"] = soft.tile([P, NB, SIDE], F32, name="mx")
                    cur["neg"] = soft.tile([P, NB, SIDE], F32, name="ng")
                    cur["exp"] = soft.tile([P, NB, SIDE, KK], F32, name="ex")
                    cur["sum"] = soft.tile([P, NB, SIDE], F32, name="sm")
                b = k // 2
                j0 = 16 * (k % 2)
                nc.vector.tensor_reduce(
                    out=cur["max"][:, b, j0 : j0 + 16],
                    in_=logit_tiles[ic][:, b, :, j0 : j0 + 16].rearrange("p l j -> p j l"),
                    axis=AX.X,
                    op=ALU.max,
                )
                nc.vector.tensor_scalar_mul(
                    out=cur["neg"][:, b, j0 : j0 + 16], in0=cur["max"][:, b, j0 : j0 + 16], scalar1=-1.0
                )
            elif k < 24:
                for col in range(8 * (k - 8), 8 * (k - 8) + 8):
                    b = col // SIDE
                    j = col % SIDE
                    nc.scalar.activation(
                        out=cur["exp"][:, b, j, :],
                        in_=logit_tiles[ic][:, b, :, j],
                        func=ACTF.Exp,
                        bias=cur["neg"][:, b, j : j + 1],
                        scale=1.0,
                        accum_out=cur["sum"][:, b, j : j + 1],
                    )
            elif k == 24:
                cur["inv"] = soft.tile([P, NB, SIDE], F32, name="rs")
                nc.vector.reciprocal(out=cur["inv"][:], in_=cur["sum"][:])
                if ic + 1 < NCHUNK:
                    load_logits(ic + 1)
            elif k < 38:
                if k % 2 == 1:
                    dy = (k - 25) // 2
                    eng = nc.vector if ic == 0 else nc.gpsimd
                    eng.tensor_tensor(
                        out=wpad[:, KW * dy : KW * dy + KW, PAD : PAD + SIDE, :],
                        in0=cur["exp"][:, :, :, KW * dy : KW * dy + KW].rearrange("p b j l -> p l j b"),
                        in1=cur["inv"][:].rearrange("p b j -> p j b").unsqueeze(1).to_broadcast([P, KW, SIDE, NB]),
                        op=ALU.mult,
                    )
            elif k == 38:
                fold_mirrored_columns()
            elif k < 52:
                if ic == 0:
                    transpose_weights(k - 39, psacc, "acc%d" % (k % NACC))
                else:
                    transpose_weights(k - 39, pswt, "wt")

        make_identity(nc, ident_bf[:])
        make_identity(nc, perm[:, 0:P])
        nc.gpsimd.memset(wpad[:], 0.0)
        nc.vector.tensor_copy(out=perm[:, P : 2 * P], in_=perm[:, 0:P])
        nc.vector.tensor_copy(out=perm[:, 2 * P : 3 * P], in_=perm[:, 0:P])

        load_logits(0)

        with tc.tile_pool(name="stage", bufs=1) as stage:
            w_sb = stage.tile([P, COUT // P, CIN], BF16)
            nc.scalar.dma_start(out=w_sb[:], in_=w3c.rearrange("(g p) c -> p g c", p=P))
            b_rows = stage.tile([P, P], BF16)
            nc.vector.memset(b_rows[:], 0.0)
            nc.scalar.dma_start(out=b_rows[0 : COUT // P, :], in_=b3c.rearrange("(g o) -> g o", g=COUT // P))
            x_sb = stage.tile([P, PACK, NB, SIDE * SIDE], BF16)
            for b in range(NB):
                nc.scalar.dma_start(out=x_sb[:, :, b, :], in_=x[b].rearrange("(t p) i j -> p t (i j)", p=P))

            w_grp = stage.tile([P, COUT // P, P, PACK], BF16, align_bytes=64)
            for g in range(COUT // P):
                wtb = pswt.tile([P, PACK, P], BF16, name="wt")
                for t in range(PACK):
                    nc.tensor.transpose(wtb[:, t, :], w_sb[:, g, P * t : P * t + P], ident_bf[:])
                nc.scalar.copy(out=w_grp[:, g], in_=wtb[:].rearrange("p t o -> p o t"))
            btp = pswt.tile([P, P], BF16, name="wt")
            nc.tensor.transpose(btp[:], b_rows[:], ident_bf[:])

            for k in range(8):
                prepare(0, k)
                prepare(0, 8 + 2 * k)
                prepare(0, 9 + 2 * k)

            nc.vector.tensor_copy(out=bias_sb[:], in_=btp[:, 0 : COUT // P])
            nc.vector.quantize_mx(
                out=wq[:].bitcast(FP8X4),
                scales=wsc[:],
                in_=w_grp[:].rearrange("p g o t -> p (g o t)"),
            )

            for part in range(4):
                xg = stage.tile([P, 256, NB, PACK], BF16, align_bytes=64, name="xg", bufs=2)
                for b in range(NB):
                    nc.vector.tensor_copy(
                        out=xg[:, :, b, :],
                        in_=x_sb[:, :, b, 256 * part : 256 * part + 256].rearrange("p t n -> p n t"),
                    )
                nc.vector.quantize_mx(
                    out=xq[:, 1024 * part : 1024 * part + 1024].bitcast(FP8X4),
                    scales=xs[:, 1024 * part : 1024 * part + 1024],
                    in_=xg[:].rearrange("p n b t -> p (n b t)"),
                )

            for k in range(24, UNITS):
                prepare(0, k)

        qvp = ctx.enter_context(tc.tile_pool(name="qvp", bufs=4))
        qap = ctx.enter_context(tc.tile_pool(name="qap", bufs=3))
        csp = ctx.enter_context(tc.tile_pool(name="csp", bufs=2))
        xcp = ctx.enter_context(tc.tile_pool(name="xcp", bufs=2))

        units = []
        for ic in range(NCHUNK):
            for half in range(2):
                for q in range(ROWS):
                    for dy in range(KW):
                        units.append((ic, half, q, dy))
        nu = len(units)
        x3_vector = []
        prod_vector = []
        prod_scalar = []
        sums = []

        def x3_pass(u, pool, name):
            ic, half, q, dy = units[u]
            a = reflect(ROWS * ic + q + dy - PAD)
            xt = pool.tile([P, HALF], F32, name=name)
            nc.tensor.matmul_mx(
                out=xt[:],
                lhsT=xq[:, P * a : P * a + P].bitcast(FP8X4),
                lhsT_scale=xs[:, P * a : P * a + P],
                rhs=wq[:, HALF * half : HALF * half + HALF].bitcast(FP8X4),
                rhs_scale=wsc[:, HALF * half : HALF * half + HALF],
                start=True,
                stop=True,
            )
            return xt

        def vector_part(u):
            ic, half, q, dy = units[u]
            h0 = NHEAD * q + HEADS * half
            qv = qvp.tile([P, DX_VEC, HALF], F32, name="qv")
            nc.vector.tensor_tensor(
                out=qv[:].rearrange("p d (h c) -> p d h c", c=SP),
                in0=x3_vector[u][:]
                .rearrange("p (h c) -> p h c", c=SP)
                .unsqueeze(1)
                .to_broadcast([P, DX_VEC, HEADS, SP]),
                in1=weight_tiles[ic][:, KW * dy : KW * dy + DX_VEC, h0 : h0 + HEADS]
                .unsqueeze(3)
                .to_broadcast([P, DX_VEC, HEADS, SP]),
                op=ALU.mult,
            )
            prod_vector.append(qv)

        def scalar_part(u):
            ic, half, q, dy = units[u]
            h0 = NHEAD * q + HEADS * half
            xb = x3_pass(u, psb, "xb")
            xc = xcp.tile([P, HALF], F32, name="xc")
            nc.scalar.copy(out=xc[:], in_=xb[:])
            if dy == 0:
                qa = csp.tile([P, DX_SCA, HALF], F32, name="cs")
                sums.append(qa)
            else:
                qa = qap.tile([P, DX_SCA, HALF], F32, name="qa")
            for d in range(DX_SCA):
                for h in range(HEADS):
                    nc.scalar.activation(
                        out=qa[:, d, SP * h : SP * h + SP],
                        in_=xc[:, SP * h : SP * h + SP],
                        func=ACTF.Copy,
                        scale=weight_tiles[ic][:, KW * dy + DX_VEC + d, h0 + h : h0 + h + 1],
                    )
            if 0 < dy < DY_SUM:
                nc.gpsimd.tensor_tensor(out=sums[-1][:], in0=sums[-1][:], in1=qa[:], op=ALU.add)
            prod_scalar.append(qa)

        def add_up(u, accs):
            dy = units[u][3]
            terms = []
            for dx in range(DX_VEC):
                terms.append((dx, prod_vector[u][:, dx, :]))
            if dy >= DY_SUM:
                for d in range(DX_SCA):
                    terms.append((DX_VEC + d, prod_scalar[u][:, d, :]))
            if dy == KW - 1:
                for d in range(DX_SCA):
                    terms.append((DX_VEC + d, sums[u // KW][:, d, :]))
            for g in range(NACC):
                for n, (dx, term) in enumerate(terms):
                    shift = NB * (dx - PAD)
                    nc.tensor.matmul(
                        out=accs[g][:],
                        lhsT=term[:, P * g : P * g + P],
                        rhs=perm[:, P + shift : 2 * P + shift],
                        start=(dy == 0 and n == 0),
                        stop=(dy == KW - 1 and n == len(terms) - 1),
                        is_transpose=True,
                    )

        x3_vector.append(x3_pass(0, psa, "xa"))
        x3_vector.append(x3_pass(1, psa, "xa"))
        for v in range(3):
            scalar_part(v)
        vector_part(0)
        accs = []
        osb = None
        for u in range(nu):
            ic, half, q, dy = units[u]
            if u + 2 < nu:
                x3_vector.append(x3_pass(u + 2, psa, "xa"))
            if u + 3 < nu:
                scalar_part(u + 3)
            if u + 1 < nu:
                vector_part(u + 1)
            if dy == 0:
                accs = []
                for g in range(NACC):
                    accs.append(psacc.tile([P, P], F32, name="acc%d" % g))
            add_up(u, accs)
            if dy == KW - 1:
                if q == 0:
                    osb = outp.tile([P, NACC, NB, ROWS, SIDE], F32, name="osb")
                for g in range(NACC):
                    gg = NACC * half + g
                    nc.scalar.activation(
                        out=osb[:, g, :, q, :],
                        in_=accs[g][:].rearrange("o (j b) -> o b j", b=NB),
                        func=ACTF.Identity,
                        bias=bias_sb[:, gg : gg + 1],
                        scale=1.0,
                    )
                if q == ROWS - 1:
                    for g in range(NACC):
                        gg = NACC * half + g
                        nc.sync.dma_start(
                            out=out[:, P * gg : P * gg + P, ROWS * ic : ROWS * ic + ROWS, :].rearrange(
                                "b o q j -> o b (q j)"
                            ),
                            in_=osb[:, g].rearrange("o b q j -> o b (q j)"),
                        )
            if ic + 1 < NCHUNK:
                prepare(ic + 1, u % UNITS)
